import numpy as np
import ml_dtypes


def mxq(x, axis, fmt="e4m3"):
    dtype, down = {"e4m3": (ml_dtypes.float8_e4m3fn, 7), "e5m2": (ml_dtypes.float8_e5m2, 14)}[fmt]
    v = np.moveaxis(np.asarray(x, np.float32).astype(ml_dtypes.bfloat16).astype(np.float64), axis, -1)
    blocks = v.reshape(v.shape[:-1] + (-1, 32))
    amax = np.abs(blocks).max(-1, keepdims=True)
    byte = np.maximum(np.where(amax > 0, np.frexp(amax)[1] - 1 + 127, 0) - down, 1)
    scale = np.exp2(byte - 127.0)
    codes = (blocks / scale).astype(np.float32).astype(dtype).astype(np.float64)
    return np.moveaxis((codes * scale).reshape(v.shape), -1, axis)


WIDE = False


def mx_kscale(k):
    if not WIDE:
        return np.ones(k)
    levels = np.array([10, -10, 5, -5, 0])
    if k % 512:
        return np.exp2(np.random.permutation(np.resize(levels, k // 32))).repeat(32)
    a = np.empty((k // 512, 16))
    for p in range(k // 512):
        a[p, :8] = np.random.permutation(np.resize(levels, 8))
        for g in range(8):
            far = levels[np.abs(levels - a[p, g]) >= 10]
            a[p, g + 8] = far[np.random.randint(len(far))]
    return np.exp2(a.ravel()).repeat(32)


BF16 = ml_dtypes.bfloat16


def bf(x):
    return np.asarray(x, np.float32).astype(BF16)


def f64(x):
    return np.asarray(x).astype(np.float64)


B, S, D, H, HD = 2, 256, 2048, 16, 128
E = H * HD
HP = HD // 2


def split_heads(t):
    return t.reshape(B, S, H, HD).transpose(0, 2, 1, 3)


def apply_rope(t, cos, sin):
    t1 = t[..., 0::2]
    t2 = t[..., 1::2]
    r1 = t1 * cos - t2 * sin
    r2 = t1 * sin + t2 * cos
    return np.stack([r1, r2], axis=-1).reshape(t.shape)


def draw0():
    s = mx_kscale(D)
    ang = np.random.uniform(-np.pi, np.pi, (S, HP))
    return {"x": bf(np.random.standard_normal((B, S, D)) * s),
            "Wq": bf(np.random.standard_normal((D, E)) / np.sqrt(D) / s[:, None]),
            "Wk": bf(np.random.standard_normal((D, E)) / np.sqrt(D) / s[:, None]),
            "rope_cos": bf(np.cos(ang)),
            "rope_sin": bf(np.sin(ang))}


def core(x, Wq, Wk, rope_cos, rope_sin):
    xq = mxq(f64(x), 2, "e4m3")
    q = split_heads(xq @ mxq(f64(Wq), 0, "e4m3"))
    k = split_heads(xq @ mxq(f64(Wk), 0, "e4m3"))
    cos, sin = f64(rope_cos), f64(rope_sin)
    return apply_rope(q, cos, sin), apply_rope(k, cos, sin)


def e4m3fn_bytes(y):
    return np.clip(np.asarray(y, np.float64), -448.0, 448.0).astype(np.float32).astype(ml_dtypes.float8_e4m3fn).view(np.uint8)


def e4m3fn_values(b):
    return np.asarray(b, np.uint8).view(ml_dtypes.float8_e4m3fn).astype(np.float64)


def setup_inputs():
    d = draw0()
    x0 = np.asarray(d['Wq']).astype(np.float64)
    s = (np.max(np.abs(x0), axis=(1,), keepdims=True) / 448.0).astype(np.float32)
    out = {}
    for k, v in d.items():
        if k == 'Wq':
            out['Wq_bytes'] = e4m3fn_bytes(x0 / s.astype(np.float64))
            out['Wq_scale'] = s
        else:
            out[k] = v
    return out


def reference(x, Wq_bytes, Wq_scale, Wk, rope_cos, rope_sin):
    return core(x, e4m3fn_values(Wq_bytes) * Wq_scale.astype(np.float64), Wk, rope_cos, rope_sin)

@@ -1,0 +1,152 @@
+from contextlib import ExitStack
+
+import concourse.mybir as mybir
+from concourse.masks import make_identity
+
+F32 = mybir.dt.float32
+BF16 = mybir.dt.bfloat16
+U32 = mybir.dt.uint32
+U8 = mybir.dt.uint8
+FP8 = mybir.dt.float8_e4m3fn
+FP8X4 = mybir.dt.float8_e4m3fn_x4
+ALU = mybir.AluOpType
+ACT = mybir.ActivationFunctionType
+
+B, S, D, H, HD = 2, 256, 2048, 16, 128
+E = H * HD
+FLOPS = 2 * (B * S) * D * (2 * E)
+
+P = 128
+PACK = 4
+KP = P * PACK
+NG = D // KP
+NC = 512
+NJ = E // NC
+NM = (B * S) // P
+HC = NC // HD
+
+
+def tile_llamaattention_pa_kernel(tc, x, Wq_bytes, Wq_scale, Wk, rope_cos, rope_sin, out_0, out_1):
+    nc = tc.nc
+    with ExitStack() as ctx:
+        const = ctx.enter_context(tc.tile_pool(name="const", bufs=1))
+        res = ctx.enter_context(tc.tile_pool(name="res", bufs=1))
+        work = ctx.enter_context(tc.tile_pool(name="work", bufs=2))
+        psum = ctx.enter_context(tc.psum_pool(name="psum", bufs=8))
+
+        scl = const.tile([P, NG, PACK], F32, name="scl")
+        nc.sync.dma_start(out=scl[:], in_=Wq_scale.rearrange("(g p t) o -> p g (t o)", p=P, t=PACK))
+        wq_v = Wq_bytes.rearrange("(g p t) n -> g p t n", p=P, t=PACK)
+        wk_v = Wk.rearrange("(g p t) n -> g p t n", p=P, t=PACK)
+        qb = {}
+        kr = {}
+
+        def load_q(j, g):
+            t = res.tile([P, PACK, NC], U8, name="qbytes%d_%d" % (j, g))
+            nc.sync.dma_start(out=t[:], in_=wq_v[g, :, :, j * NC:(j + 1) * NC])
+            qb[(j, g)] = t
+
+        def load_k(j, g):
+            t = res.tile([P, PACK, NC], BF16, name="kraw%d_%d" % (j, g))
+            nc.sync.dma_start(out=t[:], in_=wk_v[g, :, :, j * NC:(j + 1) * NC])
+            kr[(j, g)] = t
+
+        load_q(0, 0)
+        load_k(0, 0)
+        x_sb = res.tile([P, B, 2, D], BF16, name="x_sb")
+        for b in range(B):
+            nc.sync.dma_start(out=x_sb[:, b, :, :], in_=x[b].rearrange("(p e) k -> p e k", e=2))
+        cos_sb = const.tile([P, 2, HD // 2], BF16, name="cos_sb")
+        sin_sb = const.tile([P, 2, HD // 2], BF16, name="sin_sb")
+        nc.sync.dma_start(out=cos_sb[:], in_=rope_cos.rearrange("(p e) i -> p e i", e=2))
+        nc.sync.dma_start(out=sin_sb[:], in_=rope_sin.rearrange("(p e) i -> p e i", e=2))
+        for g in range(1, NG):
+            load_k(0, g)
+        for g in range(1, NG):
+            load_q(0, g)
+        for j in range(1, NJ):
+            for g in range(NG):
+                load_k(j, g)
+            for g in range(NG):
+                load_q(j, g)
+
+        warm = const.tile([P, 1], F32, name="warm")
+        warm2 = const.tile([P, 1], F32, name="warm2")
+        nc.vector.memset(warm[:], 0.0)
+        nc.scalar.activation(out=warm2[:], in_=warm[:], func=ACT.Copy)
+        ident = const.tile([P, P], F32, name="ident")
+        make_identity(nc, ident[:])
+        c2 = const.tile([P, 2, HD // 2, 2], F32, name="c2")
+        s2 = const.tile([P, 2, HD // 2, 2], F32, name="s2")
+        nc.gpsimd.tensor_copy(out=c2[:, :, :, 0], in_=cos_sb[:])
+        nc.gpsimd.tensor_copy(out=c2[:, :, :, 1], in_=cos_sb[:])
+        nc.gpsimd.tensor_scalar(out=s2[:, :, :, 0], in0=sin_sb[:], scalar1=-1.0, scalar2=None, op0=ALU.mult)
+        nc.gpsimd.tensor_copy(out=s2[:, :, :, 1], in_=sin_sb[:])
+
+        xc = res.tile([P, NG, NM * P], U32, name="xc", align_bytes=64)
+        xs = res.tile([P, NG, NM * P], U8, name="xs", align_bytes=64)
+        for g in range(NG):
+            xg = work.tile([P, NM * P * PACK], BF16, name="xg", tag="xg", align_bytes=64)
+            xgw = xg[:].bitcast(F32).rearrange("p (m r u) -> p m r u", m=NM, u=2)
+            for b in range(B):
+                xt = psum.tile([P, 2, 2, P], F32, name="xt", tag="bank")
+                for e in range(2):
+                    words = x_sb[:, b, e, :].bitcast(F32)
+                    for u in range(2):
+                        nc.tensor.transpose(xt[:, e, u, :], words[:, 256 * g + u:256 * (g + 1):2], ident[:])
+                nc.vector.tensor_copy(out=xgw[:, 2 * b:2 * b + 2, :, :], in_=xt[:].rearrange("p e u r -> p e r u"))
+            nc.vector.quantize_mx(out=xc[:, g, :].bitcast(FP8X4), scales=xs[:, g, :], in_=xg[:])
+
+        def prep_k(j):
+            wc = work.tile([P, NG, NC], U32, name="kc", tag="kc", align_bytes=64)
+            ws = work.tile([P, NG, NC], U8, name="ks", tag="ks", align_bytes=64)
+            for g in range(NG):
+                il = work.tile([P, NC, PACK], BF16, name="ilk", tag="ilk", bufs=3, align_bytes=64)
+                nc.vector.tensor_copy(out=il[:], in_=kr[(j, g)][:].rearrange("p t c -> p c t"))
+                nc.vector.quantize_mx(out=wc[:, g, :].bitcast(FP8X4), scales=ws[:, g, :],
+                                      in_=il[:].rearrange("p c t -> p (c t)"))
+            return wc, ws
+
+        def prep_q(j):
+            wc = work.tile([P, NG, NC], U32, name="qc", tag="qc", align_bytes=64)
+            ws = work.tile([P, NG, NC], U8, name="qs", tag="qs", align_bytes=64)
+            for g in range(NG):
+                wid = work.tile([P, PACK, NC], BF16, name="wid", tag="wid")
+                for t in range(PACK):
+                    nc.scalar.activation(out=wid[:, t, :], in_=qb[(j, g)][:, t, :].bitcast(FP8),
+                                         func=ACT.Copy, scale=scl[:, g, t:t + 1])
+                il = work.tile([P, NC, PACK], BF16, name="ilq", tag="ilq", bufs=3, align_bytes=64)
+                nc.scalar.copy(out=il[:], in_=wid[:].rearrange("p t c -> p c t"))
+                nc.vector.quantize_mx(out=wc[:, g, :].bitcast(FP8X4), scales=ws[:, g, :],
+                                      in_=il[:].rearrange("p c t -> p (c t)"))
+            return wc, ws
+
+        def finish(j, wc, ws, out):
+            for b in range(B):
+                r = work.tile([P, HC, 2, HD], F32, name="r", tag="r", bufs=3)
+                for e in range(2):
+                    m = 2 * b + e
+                    acc = psum.tile([P, NC], F32, name="acc", tag="bank")
+                    for g in range(NG):
+                        nc.tensor.matmul_mx(out=acc[:],
+                                            lhsT=xc[:, g, m * P:(m + 1) * P].bitcast(FP8X4),
+                                            lhsT_scale=xs[:, g, m * P:(m + 1) * P],
+                                            rhs=wc[:, g, :].bitcast(FP8X4), rhs_scale=ws[:, g, :],
+                                            start=(g == 0), stop=(g == NG - 1))
+                    shp = [P, HC, HD // 2, 2]
+                    accv = acc[:].rearrange("p (h i r) -> p h i r", h=HC, r=2)
+                    pa = work.tile(shp, F32, name="pa", tag="pa", bufs=3)
+                    pb = work.tile(shp, F32, name="pb", tag="pb", bufs=3)
+                    nc.vector.tensor_tensor(out=pa[:], in0=accv, in1=c2[:, e].unsqueeze(1).to_broadcast(shp), op=ALU.mult)
+                    nc.vector.tensor_tensor(out=pb[:], in0=accv[:, :, :, ::-1], in1=s2[:, e].unsqueeze(1).to_broadcast(shp), op=ALU.mult)
+                    eng = nc.vector if m == NM - 1 else nc.gpsimd
+                    eng.tensor_tensor(out=r[:, :, e, :], in0=pa[:].rearrange("p h i r -> p h (i r)"),
+                                      in1=pb[:].rearrange("p h i r -> p h (i r)"), op=ALU.add)
+                nc.sync.dma_start(out=out[b, j * HC:(j + 1) * HC].rearrange("h (p e) d -> p h (e d)", e=2),
+                                  in_=r[:].rearrange("p h e d -> p h (e d)"))
+
+        for j in range(NJ):
+            kc, ks = prep_k(j)
+            finish(j, kc, ks, out_1)
+            qc, qs = prep_q(j)
+            finish(j, qc, qs, out_0)

@@ -25,50 +25,149 @@ NJ = E // NC
 NM = (B * S) // P
 HC = NC // HD
 
+Q_ON_VECTOR = ((0, 0), (0, 1), (0, 2), (0, 3), (1, 3), (2, 3), (3, 3))
+COVER = (3, 3, 3, 3, 4, 0, 0, 0)
+VADD_COVERED = (3,)
+VADD_BARE = (2, 3)
+
 
 def tile_llamaattention_pa_kernel(tc, x, Wq_bytes, Wq_scale, Wk, rope_cos, rope_sin, out_0, out_1):
     nc = tc.nc
+    outs = {"q": out_0, "k": out_1}
     with ExitStack() as ctx:
         const = ctx.enter_context(tc.tile_pool(name="const", bufs=1))
-        res = ctx.enter_context(tc.tile_pool(name="res", bufs=1))
-        work = ctx.enter_context(tc.tile_pool(name="work", bufs=2))
-        psum = ctx.enter_context(tc.psum_pool(name="psum", bufs=8))
+        raw = ctx.enter_context(tc.tile_pool(name="raw", bufs=12))
+        work = ctx.enter_context(tc.tile_pool(name="work", bufs=3))
+        psum = ctx.enter_context(tc.psum_pool(name="psum", bufs=4))
+        ctx.enter_context(tc.manual_schedule())
 
-        scl = const.tile([P, NG, PACK], F32, name="scl")
-        nc.sync.dma_start(out=scl[:], in_=Wq_scale.rearrange("(g p t) o -> p g (t o)", p=P, t=PACK))
         wq_v = Wq_bytes.rearrange("(g p t) n -> g p t n", p=P, t=PACK)
         wk_v = Wk.rearrange("(g p t) n -> g p t n", p=P, t=PACK)
-        qb = {}
-        kr = {}
+        src = {}
+        il = {}
+        codes = {}
+        stage = {}
+        acc = {}
+        prod = {}
+        res = {}
 
-        def load_q(j, g):
-            t = res.tile([P, PACK, NC], U8, name="qbytes%d_%d" % (j, g))
+        def ld_q(j, g):
+            t = raw.tile([P, PACK, NC], U8, name="qbytes", tag="qbytes")
             nc.sync.dma_start(out=t[:], in_=wq_v[g, :, :, j * NC:(j + 1) * NC])
-            qb[(j, g)] = t
+            src[("b", j, g)] = t
 
-        def load_k(j, g):
-            t = res.tile([P, PACK, NC], BF16, name="kraw%d_%d" % (j, g))
+        def ld_k(j, g):
+            t = raw.tile([P, PACK, NC], BF16, name="kraw", tag="kraw")
             nc.sync.dma_start(out=t[:], in_=wk_v[g, :, :, j * NC:(j + 1) * NC])
-            kr[(j, g)] = t
+            src[("k", j, g)] = t
 
-        load_q(0, 0)
-        load_k(0, 0)
-        x_sb = res.tile([P, B, 2, D], BF16, name="x_sb")
-        for b in range(B):
-            nc.sync.dma_start(out=x_sb[:, b, :, :], in_=x[b].rearrange("(p e) k -> p e k", e=2))
+        def widen(j, g):
+            t = work.tile([P, PACK, NC], BF16, name="wid", tag="wid")
+            for k in range(PACK):
+                nc.scalar.activation(out=t[:, k, :], in_=src[("b", j, g)][:, k, :].bitcast(FP8),
+                                     func=ACT.Copy, scale=scl[:, g, k:k + 1])
+            src[("q", j, g)] = t
+
+        def new_il(w, j, g):
+            t = work.tile([P, NC, PACK], BF16, name="il" + w, tag="il" + w, bufs=(4 if w == "k" else 3), align_bytes=64)
+            il[(w, j, g)] = t
+            return t
+
+        def inter(eng, w, j, g):
+            t = new_il(w, j, g)
+            view = src[(w, j, g)][:].rearrange("p t c -> p c t")
+            if eng == "V":
+                nc.vector.tensor_copy(out=t[:], in_=view)
+            else:
+                nc.scalar.copy(out=t[:], in_=view)
+
+        def pe_inter(j, g, h):
+            t = psum.tile([P, NC // 2, PACK], BF16, name="stg", tag="stg")
+            for q in range(2):
+                c0 = h * 256 + q * 128
+                nc.tensor.matmul(out=t[:, q * 128:(q + 1) * 128, :], lhsT=identb[:],
+                                 rhs=src[("k", j, g)][:, :, c0:c0 + 128].rearrange("p t c -> p c t"),
+                                 start=True, stop=True)
+            stage[(j, g, h)] = t
+
+        def empty(eng, j, g, h):
+            if h == 0:
+                new_il("k", j, g)
+            dst = il[("k", j, g)][:, h * 256:(h + 1) * 256, :]
+            if eng == "V":
+                nc.vector.tensor_copy(out=dst, in_=stage[(j, g, h)][:])
+            else:
+                nc.scalar.copy(out=dst, in_=stage[(j, g, h)][:])
+
+        def quant(w, j, g):
+            if g == 0:
+                c = work.tile([P, NG, NC], U32, name=w + "c", tag=w + "c", bufs=2, align_bytes=64)
+                s = work.tile([P, NG, NC], U8, name=w + "s", tag=w + "s", bufs=2, align_bytes=64)
+                codes[(w, j)] = (c, s)
+            c, s = codes[(w, j)]
+            nc.vector.quantize_mx(out=c[:, g, :].bitcast(FP8X4), scales=s[:, g, :],
+                                  in_=il[(w, j, g)][:].rearrange("p c t -> p (c t)"))
+
+        def mm(w, j, m):
+            t = psum.tile([P, NC], F32, name="acc", tag="acc")
+            c, s = codes[(w, j)]
+            for g in range(NG):
+                nc.tensor.matmul_mx(out=t[:], lhsT=xc[:, g, m * P:(m + 1) * P].bitcast(FP8X4),
+                                    lhsT_scale=xs[:, g, m * P:(m + 1) * P],
+                                    rhs=c[:, g, :].bitcast(FP8X4), rhs_scale=s[:, g, :],
+                                    start=(g == 0), stop=(g == NG - 1))
+            acc[(w, j, m)] = t
+
+        shp = [P, HC, HD // 2, 2]
+
+        def products(w, j, m):
+            e = m % 2
+            a = acc[(w, j, m)][:].rearrange("p (h i r) -> p h i r", h=HC, r=2)
+            pa = work.tile(shp, F32, name="pa", tag="pa")
+            pb = work.tile(shp, F32, name="pb", tag="pb")
+            nc.vector.tensor_tensor(out=pa[:], in0=a, in1=c2[:, e].unsqueeze(1).to_broadcast(shp), op=ALU.mult)
+            nc.vector.tensor_tensor(out=pb[:], in0=a[:, :, :, ::-1], in1=s2[:, e].unsqueeze(1).to_broadcast(shp), op=ALU.mult)
+            prod[(w, j, m)] = (pa, pb)
+
+        def add(eng, w, j, m):
+            b, e = m // 2, m % 2
+            if e == 0:
+                res[(w, j, b)] = work.tile([P, HC, 2, HD], F32, name="r", tag="r")
+            pa, pb = prod[(w, j, m)]
+            eng.tensor_tensor(out=res[(w, j, b)][:, :, e, :], in0=pa[:].rearrange("p h i r -> p h (i r)"),
+                              in1=pb[:].rearrange("p h i r -> p h (i r)"), op=ALU.add)
+
+        def store(w, j, b):
+            nc.sync.dma_start(out=outs[w][b, j * HC:(j + 1) * HC].rearrange("h (p e) d -> p h (e d)", e=2),
+                              in_=res[(w, j, b)][:].rearrange("p h e d -> p h (e d)"))
+
+        scl = const.tile([P, NG, PACK], F32, name="scl")
+        x_sb = const.tile([P, B, 2, D], BF16, name="x_sb")
         cos_sb = const.tile([P, 2, HD // 2], BF16, name="cos_sb")
         sin_sb = const.tile([P, 2, HD // 2], BF16, name="sin_sb")
+
+        def ld_x(b):
+            nc.sync.dma_start(out=x_sb[:, b, :, :], in_=x[b].rearrange("(p e) k -> p e k", e=2))
+
+        nc.sync.dma_start(out=scl[:], in_=Wq_scale.rearrange("(g p t) o -> p g (t o)", p=P, t=PACK))
+        ld_k(0, 0)
+        ld_q(0, 0)
+        ld_q(0, 1)
+        ld_k(0, 1)
+        ld_x(0)
+        ld_k(0, 2)
+        ld_q(0, 2)
+        ld_x(1)
+        ld_k(0, 3)
+        ld_q(0, 3)
         nc.sync.dma_start(out=cos_sb[:], in_=rope_cos.rearrange("(p e) i -> p e i", e=2))
         nc.sync.dma_start(out=sin_sb[:], in_=rope_sin.rearrange("(p e) i -> p e i", e=2))
-        for g in range(1, NG):
-            load_k(0, g)
-        for g in range(1, NG):
-            load_q(0, g)
-        for j in range(1, NJ):
+        for j in (1, 2):
             for g in range(NG):
-                load_k(j, g)
+                ld_k(j, g)
             for g in range(NG):
-                load_q(j, g)
+                ld_q(j, g)
+        late_loads = [(ld_k, 3), (ld_q, 3)]
 
         warm = const.tile([P, 1], F32, name="warm")
         warm2 = const.tile([P, 1], F32, name="warm2")
@@ -76,6 +175,8 @@ def tile_llamaattention_pa_kernel(tc, x, Wq_bytes, Wq_scale, Wk, rope_cos, rope_
         nc.scalar.activation(out=warm2[:], in_=warm[:], func=ACT.Copy)
         ident = const.tile([P, P], F32, name="ident")
         make_identity(nc, ident[:])
+        identb = const.tile([P, P], BF16, name="identb")
+        make_identity(nc, identb[:])
         c2 = const.tile([P, 2, HD // 2, 2], F32, name="c2")
         s2 = const.tile([P, 2, HD // 2, 2], F32, name="s2")
         nc.gpsimd.tensor_copy(out=c2[:, :, :, 0], in_=cos_sb[:])
@@ -83,70 +184,106 @@ def tile_llamaattention_pa_kernel(tc, x, Wq_bytes, Wq_scale, Wk, rope_cos, rope_
         nc.gpsimd.tensor_scalar(out=s2[:, :, :, 0], in0=sin_sb[:], scalar1=-1.0, scalar2=None, op0=ALU.mult)
         nc.gpsimd.tensor_copy(out=s2[:, :, :, 1], in_=sin_sb[:])
 
-        xc = res.tile([P, NG, NM * P], U32, name="xc", align_bytes=64)
-        xs = res.tile([P, NG, NM * P], U8, name="xs", align_bytes=64)
+        xc = const.tile([P, NG, NM * P], U32, name="xc", align_bytes=64)
+        xs = const.tile([P, NG, NM * P], U8, name="xs", align_bytes=64)
+        xg = {}
+
+        def x_turn(b, g):
+            xt = psum.tile([P, 2, 2, P], F32, name="xt", tag="acc")
+            for e in range(2):
+                words = x_sb[:, b, e, :].bitcast(F32)
+                for u in range(2):
+                    nc.tensor.transpose(xt[:, e, u, :], words[:, 256 * g + u:256 * (g + 1):2], ident[:])
+            t = work.tile([P, 2 * P * PACK], BF16, name="xg", tag="xg", bufs=4, align_bytes=64)
+            nc.scalar.copy(out=t[:].bitcast(F32).rearrange("p (e r u) -> p e r u", e=2, u=2),
+                           in_=xt[:].rearrange("p e u r -> p e r u"))
+            xg[(b, g)] = t
+
+        def x_quant(b, g):
+            cols = slice(b * 2 * P, (b + 1) * 2 * P)
+            nc.vector.quantize_mx(out=xc[:, g, cols].bitcast(FP8X4), scales=xs[:, g, cols], in_=xg[(b, g)][:])
+
+        widen(0, 0)
+        widen(0, 1)
+        inter("V", "k", 0, 0)
+        inter("V", "q", 0, 0)
+        quant("k", 0, 0)
+        inter("V", "k", 0, 1)
+        quant("q", 0, 0)
+        inter("V", "q", 0, 1)
+        quant("k", 0, 1)
         for g in range(NG):
-            xg = work.tile([P, NM * P * PACK], BF16, name="xg", tag="xg", align_bytes=64)
-            xgw = xg[:].bitcast(F32).rearrange("p (m r u) -> p m r u", m=NM, u=2)
-            for b in range(B):
-                xt = psum.tile([P, 2, 2, P], F32, name="xt", tag="bank")
-                for e in range(2):
-                    words = x_sb[:, b, e, :].bitcast(F32)
-                    for u in range(2):
-                        nc.tensor.transpose(xt[:, e, u, :], words[:, 256 * g + u:256 * (g + 1):2], ident[:])
-                nc.vector.tensor_copy(out=xgw[:, 2 * b:2 * b + 2, :, :], in_=xt[:].rearrange("p e u r -> p e r u"))
-            nc.vector.quantize_mx(out=xc[:, g, :].bitcast(FP8X4), scales=xs[:, g, :], in_=xg[:])
+            x_turn(0, g)
+        widen(0, 2)
+        inter("V", "k", 0, 2)
+        quant("q", 0, 1)
+        x_quant(0, 0)
+        x_quant(0, 1)
+        quant("k", 0, 2)
+        x_quant(0, 2)
+        x_quant(0, 3)
+        inter("V", "q", 0, 2)
+        for g in range(NG):
+            x_turn(1, g)
+        widen(0, 3)
+        inter("V", "k", 0, 3)
+        quant("q", 0, 2)
+        x_quant(1, 0)
+        x_quant(1, 1)
+        quant("k", 0, 3)
+        x_quant(1, 2)
+        x_quant(1, 3)
+        inter("V", "q", 0, 3)
+        for g in range(NG):
+            for h in range(2):
+                pe_inter(1, g, h)
+                empty("S", 1, g, h)
+        quant("k", 1, 0)
+        quant("q", 0, 3)
+        for g in range(1, NG):
+            quant("k", 1, g)
 
-        def prep_k(j):
-            wc = work.tile([P, NG, NC], U32, name="kc", tag="kc", align_bytes=64)
-            ws = work.tile([P, NG, NC], U8, name="ks", tag="ks", align_bytes=64)
-            for g in range(NG):
-                il = work.tile([P, NC, PACK], BF16, name="ilk", tag="ilk", bufs=3, align_bytes=64)
-                nc.vector.tensor_copy(out=il[:], in_=kr[(j, g)][:].rearrange("p t c -> p c t"))
-                nc.vector.quantize_mx(out=wc[:, g, :].bitcast(FP8X4), scales=ws[:, g, :],
-                                      in_=il[:].rearrange("p c t -> p (c t)"))
-            return wc, ws
-
-        def prep_q(j):
-            wc = work.tile([P, NG, NC], U32, name="qc", tag="qc", align_bytes=64)
-            ws = work.tile([P, NG, NC], U8, name="qs", tag="qs", align_bytes=64)
-            for g in range(NG):
-                wid = work.tile([P, PACK, NC], BF16, name="wid", tag="wid")
-                for t in range(PACK):
-                    nc.scalar.activation(out=wid[:, t, :], in_=qb[(j, g)][:, t, :].bitcast(FP8),
-                                         func=ACT.Copy, scale=scl[:, g, t:t + 1])
-                il = work.tile([P, NC, PACK], BF16, name="ilq", tag="ilq", bufs=3, align_bytes=64)
-                nc.scalar.copy(out=il[:], in_=wid[:].rearrange("p t c -> p c t"))
-                nc.vector.quantize_mx(out=wc[:, g, :].bitcast(FP8X4), scales=ws[:, g, :],
-                                      in_=il[:].rearrange("p c t -> p (c t)"))
-            return wc, ws
-
-        def finish(j, wc, ws, out):
-            for b in range(B):
-                r = work.tile([P, HC, 2, HD], F32, name="r", tag="r", bufs=3)
-                for e in range(2):
-                    m = 2 * b + e
-                    acc = psum.tile([P, NC], F32, name="acc", tag="bank")
-                    for g in range(NG):
-                        nc.tensor.matmul_mx(out=acc[:],
-                                            lhsT=xc[:, g, m * P:(m + 1) * P].bitcast(FP8X4),
-                                            lhsT_scale=xs[:, g, m * P:(m + 1) * P],
-                                            rhs=wc[:, g, :].bitcast(FP8X4), rhs_scale=ws[:, g, :],
-                                            start=(g == 0), stop=(g == NG - 1))
-                    shp = [P, HC, HD // 2, 2]
-                    accv = acc[:].rearrange("p (h i r) -> p h i r", h=HC, r=2)
-                    pa = work.tile(shp, F32, name="pa", tag="pa", bufs=3)
-                    pb = work.tile(shp, F32, name="pb", tag="pb", bufs=3)
-                    nc.vector.tensor_tensor(out=pa[:], in0=accv, in1=c2[:, e].unsqueeze(1).to_broadcast(shp), op=ALU.mult)
-                    nc.vector.tensor_tensor(out=pb[:], in0=accv[:, :, :, ::-1], in1=s2[:, e].unsqueeze(1).to_broadcast(shp), op=ALU.mult)
-                    eng = nc.vector if m == NM - 1 else nc.gpsimd
-                    eng.tensor_tensor(out=r[:, :, e, :], in0=pa[:].rearrange("p h i r -> p h (i r)"),
-                                      in1=pb[:].rearrange("p h i r -> p h (i r)"), op=ALU.add)
-                nc.sync.dma_start(out=out[b, j * HC:(j + 1) * HC].rearrange("h (p e) d -> p h (e d)", e=2),
-                                  in_=r[:].rearrange("p h e d -> p h (e d)"))
-
-        for j in range(NJ):
-            kc, ks = prep_k(j)
-            finish(j, kc, ks, out_1)
-            qc, qs = prep_q(j)
-            finish(j, qc, qs, out_0)
+        seq = [(w, j) for j in range(NJ) for w in ("k", "q")]
+        banks = [(j, g, h) for j in (2, 3) for g in range(NG) for h in range(2)]
+        for i in range(len(seq)):
+            w, j = seq[i]
+            cover = banks[:COVER[i]]
+            banks = banks[COVER[i]:]
+            for m in range(NM):
+                mm(w, j, m)
+            for bk in cover:
+                pe_inter(*bk)
+            nxt = seq[i + 2] if i + 2 < len(seq) else None
+            if nxt and nxt[0] == "q":
+                for g in range(NG):
+                    widen(nxt[1], g)
+                    if (nxt[1], g) not in Q_ON_VECTOR:
+                        inter("S", "q", nxt[1], g)
+            vadd = VADD_COVERED if cover else VADD_BARE
+            for m in range(NM):
+                products(w, j, m)
+                if m not in vadd:
+                    add(nc.gpsimd, w, j, m)
+                    if m % 2 == 1:
+                        store(w, j, m // 2)
+            for bk in cover:
+                empty("V", *bk)
+            for m in vadd:
+                add(nc.vector, w, j, m)
+                if m % 2 == 1:
+                    store(w, j, m // 2)
+            if late_loads:
+                fn, jj = late_loads.pop(0)
+                for g in range(NG):
+                    fn(jj, g)
+            kq = [bk[:2] for bk in cover if bk[2] == 1]
+            if nxt and nxt[0] == "q":
+                for g in range(NG):
+                    if (nxt[1], g) in Q_ON_VECTOR:
+                        inter("V", "q", nxt[1], g)
+                        for u in kq:
+                            quant("k", *u)
+                        kq = []
+                    quant("q", nxt[1], g)
+            for u in kq:
+                quant("k", *u)

@@ -68,18 +68,18 @@ def tile_llamaattention_pa_kernel(tc, x, Wq_bytes, Wq_scale, Wk, rope_cos, rope_
                                      func=ACT.Copy, scale=scl[:, g, k:k + 1])
             src[("q", j, g)] = t
 
-        def new_il(w, j, g):
-            t = work.tile([P, NC, PACK], BF16, name="il" + w, tag="il" + w, bufs=(4 if w == "k" else 3), align_bytes=64)
-            il[(w, j, g)] = t
-            return t
+        def il_of(w, j, g):
+            if (w, j, g // 2) not in il:
+                il[(w, j, g // 2)] = work.tile([P, 2, NC, PACK], BF16, name="il" + w, tag="il" + w, bufs=2, align_bytes=64)
+            return il[(w, j, g // 2)]
 
         def inter(eng, w, j, g):
-            t = new_il(w, j, g)
+            t = il_of(w, j, g)
             view = src[(w, j, g)][:].rearrange("p t c -> p c t")
             if eng == "V":
-                nc.vector.tensor_copy(out=t[:], in_=view)
+                nc.vector.tensor_copy(out=t[:, g % 2], in_=view)
             else:
-                nc.scalar.copy(out=t[:], in_=view)
+                nc.scalar.copy(out=t[:, g % 2], in_=view)
 
         def pe_inter(j, g, h):
             t = psum.tile([P, NC // 2, PACK], BF16, name="stg", tag="stg")
@@ -91,51 +91,49 @@ def tile_llamaattention_pa_kernel(tc, x, Wq_bytes, Wq_scale, Wk, rope_cos, rope_
             stage[(j, g, h)] = t
 
         def empty(eng, j, g, h):
-            if h == 0:
-                new_il("k", j, g)
-            dst = il[("k", j, g)][:, h * 256:(h + 1) * 256, :]
+            dst = il_of("k", j, g)[:, g % 2, h * 256:(h + 1) * 256, :]
             if eng == "V":
                 nc.vector.tensor_copy(out=dst, in_=stage[(j, g, h)][:])
             else:
                 nc.scalar.copy(out=dst, in_=stage[(j, g, h)][:])
 
-        def quant(w, j, g):
-            if g == 0:
+        def quant(w, j, gg):
+            if gg == 0:
                 c = work.tile([P, NG, NC], U32, name=w + "c", tag=w + "c", bufs=2, align_bytes=64)
                 s = work.tile([P, NG, NC], U8, name=w + "s", tag=w + "s", bufs=2, align_bytes=64)
                 codes[(w, j)] = (c, s)
             c, s = codes[(w, j)]
-            nc.vector.quantize_mx(out=c[:, g, :].bitcast(FP8X4), scales=s[:, g, :],
-                                  in_=il[(w, j, g)][:].rearrange("p c t -> p (c t)"))
+            nc.vector.quantize_mx(out=c[:, 2 * gg:2 * gg + 2, :].rearrange("p g c -> p (g c)").bitcast(FP8X4),
+                                  scales=s[:, 2 * gg:2 * gg + 2, :].rearrange("p g c -> p (g c)"),
+                                  in_=il[(w, j, gg)][:].rearrange("p g c t -> p (g c t)"))
 
         def mm(w, j, m):
             t = psum.tile([P, NC], F32, name="acc", tag="acc")
             c, s = codes[(w, j)]
+            b, e = m // 2, m % 2
             for g in range(NG):
-                nc.tensor.matmul_mx(out=t[:], lhsT=xc[:, g, m * P:(m + 1) * P].bitcast(FP8X4),
-                                    lhsT_scale=xs[:, g, m * P:(m + 1) * P],
+                nc.tensor.matmul_mx(out=t[:], lhsT=xc[:, b, g, e * P:(e + 1) * P].bitcast(FP8X4),
+                                    lhsT_scale=xs[:, b, g, e * P:(e + 1) * P],
                                     rhs=c[:, g, :].bitcast(FP8X4), rhs_scale=s[:, g, :],
                                     start=(g == 0), stop=(g == NG - 1))
             acc[(w, j, m)] = t
 
-        shp = [P, HC, HD // 2, 2]
-
         def products(w, j, m):
-            e = m % 2
-            a = acc[(w, j, m)][:].rearrange("p (h i r) -> p h i r", h=HC, r=2)
-            pa = work.tile(shp, F32, name="pa", tag="pa")
-            pb = work.tile(shp, F32, name="pb", tag="pb")
-            nc.vector.tensor_tensor(out=pa[:], in0=a, in1=c2[:, e].unsqueeze(1).to_broadcast(shp), op=ALU.mult)
-            nc.vector.tensor_tensor(out=pb[:], in0=a[:, :, :, ::-1], in1=s2[:, e].unsqueeze(1).to_broadcast(shp), op=ALU.mult)
-            prod[(w, j, m)] = (pa, pb)
+            shp = [P, 2, HC, HD]
+            t = work.tile(shp, F32, name="pab", tag="pab")
+            nc.vector.tensor_tensor(out=t[:], in0=tab[:, m % 2].unsqueeze(2).to_broadcast(shp),
+                                    in1=acc[(w, j, m)][:].rearrange("p (h d) -> p h d", h=HC).unsqueeze(1).to_broadcast(shp),
+                                    op=ALU.mult)
+            prod[(w, j, m)] = t
 
         def add(eng, w, j, m):
             b, e = m // 2, m % 2
             if e == 0:
                 res[(w, j, b)] = work.tile([P, HC, 2, HD], F32, name="r", tag="r")
-            pa, pb = prod[(w, j, m)]
-            eng.tensor_tensor(out=res[(w, j, b)][:, :, e, :], in0=pa[:].rearrange("p h i r -> p h (i r)"),
-                              in1=pb[:].rearrange("p h i r -> p h (i r)"), op=ALU.add)
+            t = prod[(w, j, m)]
+            eng.tensor_tensor(out=res[(w, j, b)][:, :, e, :].rearrange("p h (i r) -> p h i r", r=2),
+                              in0=t[:, 0].rearrange("p h (i r) -> p h i r", r=2),
+                              in1=t[:, 1].rearrange("p h (i r) -> p h i r", r=2)[:, :, :, ::-1], op=ALU.add)
 
         def store(w, j, b):
             nc.sync.dma_start(out=outs[w][b, j * HC:(j + 1) * HC].rearrange("h (p e) d -> p h (e d)", e=2),
@@ -149,7 +147,7 @@ def tile_llamaattention_pa_kernel(tc, x, Wq_bytes, Wq_scale, Wk, rope_cos, rope_
         def ld_x(b):
             nc.sync.dma_start(out=x_sb[:, b, :, :], in_=x[b].rearrange("(p e) k -> p e k", e=2))
 
-        nc.sync.dma_start(out=scl[:], in_=Wq_scale.rearrange("(g p t) o -> p g (t o)", p=P, t=PACK))
+        nc.scalar.dma_start(out=scl[:], in_=Wq_scale.rearrange("(g p t) o -> p g (t o)", p=P, t=PACK))
         ld_k(0, 0)
         ld_q(0, 0)
         ld_q(0, 1)
@@ -160,8 +158,8 @@ def tile_llamaattention_pa_kernel(tc, x, Wq_bytes, Wq_scale, Wk, rope_cos, rope_
         ld_x(1)
         ld_k(0, 3)
         ld_q(0, 3)
-        nc.sync.dma_start(out=cos_sb[:], in_=rope_cos.rearrange("(p e) i -> p e i", e=2))
-        nc.sync.dma_start(out=sin_sb[:], in_=rope_sin.rearrange("(p e) i -> p e i", e=2))
+        nc.scalar.dma_start(out=cos_sb[:], in_=rope_cos.rearrange("(p e) i -> p e i", e=2))
+        nc.scalar.dma_start(out=sin_sb[:], in_=rope_sin.rearrange("(p e) i -> p e i", e=2))
         for j in (1, 2):
             for g in range(NG):
                 ld_k(j, g)
@@ -177,71 +175,61 @@ def tile_llamaattention_pa_kernel(tc, x, Wq_bytes, Wq_scale, Wk, rope_cos, rope_
         make_identity(nc, ident[:])
         identb = const.tile([P, P], BF16, name="identb")
         make_identity(nc, identb[:])
-        c2 = const.tile([P, 2, HD // 2, 2], F32, name="c2")
-        s2 = const.tile([P, 2, HD // 2, 2], F32, name="s2")
-        nc.gpsimd.tensor_copy(out=c2[:, :, :, 0], in_=cos_sb[:])
-        nc.gpsimd.tensor_copy(out=c2[:, :, :, 1], in_=cos_sb[:])
-        nc.gpsimd.tensor_scalar(out=s2[:, :, :, 0], in0=sin_sb[:], scalar1=-1.0, scalar2=None, op0=ALU.mult)
-        nc.gpsimd.tensor_copy(out=s2[:, :, :, 1], in_=sin_sb[:])
+        tab = const.tile([P, 2, 2, HD], F32, name="tab")
+        tabv = tab[:].rearrange("p e f (i r) -> p e f i r", r=2)
+        nc.gpsimd.tensor_copy(out=tabv[:, :, 0, :, 0], in_=cos_sb[:])
+        nc.gpsimd.tensor_copy(out=tabv[:, :, 0, :, 1], in_=cos_sb[:])
+        nc.gpsimd.tensor_copy(out=tabv[:, :, 1, :, 0], in_=sin_sb[:])
+        nc.gpsimd.tensor_scalar(out=tabv[:, :, 1, :, 1], in0=sin_sb[:], scalar1=-1.0, scalar2=None, op0=ALU.mult)
 
-        xc = const.tile([P, NG, NM * P], U32, name="xc", align_bytes=64)
-        xs = const.tile([P, NG, NM * P], U8, name="xs", align_bytes=64)
+        xc = const.tile([P, B, NG, 2 * P], U32, name="xc", align_bytes=64)
+        xs = const.tile([P, B, NG, 2 * P], U8, name="xs", align_bytes=64)
         xg = {}
 
         def x_turn(b, g):
+            if g == 0:
+                xg[b] = work.tile([P, NG, 2 * P * PACK], BF16, name="xg", tag="xg", bufs=2, align_bytes=64)
             xt = psum.tile([P, 2, 2, P], F32, name="xt", tag="acc")
             for e in range(2):
                 words = x_sb[:, b, e, :].bitcast(F32)
                 for u in range(2):
                     nc.tensor.transpose(xt[:, e, u, :], words[:, 256 * g + u:256 * (g + 1):2], ident[:])
-            t = work.tile([P, 2 * P * PACK], BF16, name="xg", tag="xg", bufs=4, align_bytes=64)
-            nc.scalar.copy(out=t[:].bitcast(F32).rearrange("p (e r u) -> p e r u", e=2, u=2),
+            nc.scalar.copy(out=xg[b][:, g, :].bitcast(F32).rearrange("p (e r u) -> p e r u", e=2, u=2),
                            in_=xt[:].rearrange("p e u r -> p e r u"))
-            xg[(b, g)] = t
 
-        def x_quant(b, g):
-            cols = slice(b * 2 * P, (b + 1) * 2 * P)
-            nc.vector.quantize_mx(out=xc[:, g, cols].bitcast(FP8X4), scales=xs[:, g, cols], in_=xg[(b, g)][:])
+        def x_quant(b):
+            nc.vector.quantize_mx(out=xc[:, b].rearrange("p g c -> p (g c)").bitcast(FP8X4),
+                                  scales=xs[:, b].rearrange("p g c -> p (g c)"),
+                                  in_=xg[b][:].rearrange("p g c -> p (g c)"))
 
         widen(0, 0)
         widen(0, 1)
         inter("V", "k", 0, 0)
         inter("V", "q", 0, 0)
-        quant("k", 0, 0)
         inter("V", "k", 0, 1)
-        quant("q", 0, 0)
         inter("V", "q", 0, 1)
-        quant("k", 0, 1)
+        quant("k", 0, 0)
+        quant("q", 0, 0)
         for g in range(NG):
             x_turn(0, g)
         widen(0, 2)
         inter("V", "k", 0, 2)
-        quant("q", 0, 1)
-        x_quant(0, 0)
-        x_quant(0, 1)
-        quant("k", 0, 2)
-        x_quant(0, 2)
-        x_quant(0, 3)
+        x_quant(0)
         inter("V", "q", 0, 2)
         for g in range(NG):
             x_turn(1, g)
         widen(0, 3)
         inter("V", "k", 0, 3)
-        quant("q", 0, 2)
-        x_quant(1, 0)
-        x_quant(1, 1)
-        quant("k", 0, 3)
-        x_quant(1, 2)
-        x_quant(1, 3)
         inter("V", "q", 0, 3)
+        quant("k", 0, 1)
+        x_quant(1)
+        quant("q", 0, 1)
         for g in range(NG):
             for h in range(2):
                 pe_inter(1, g, h)
                 empty("S", 1, g, h)
         quant("k", 1, 0)
-        quant("q", 0, 3)
-        for g in range(1, NG):
-            quant("k", 1, g)
+        quant("k", 1, 1)
 
         seq = [(w, j) for j in range(NJ) for w in ("k", "q")]
         banks = [(j, g, h) for j in (2, 3) for g in range(NG) for h in range(2)]
@@ -273,17 +261,17 @@ def tile_llamaattention_pa_kernel(tc, x, Wq_bytes, Wq_scale, Wk, rope_cos, rope_
                 if m % 2 == 1:
                     store(w, j, m // 2)
             if late_loads:
-                fn, jj = late_loads.pop(0)
+                fn, jj = late_loads[0]
+                late_loads = late_loads[1:]
                 for g in range(NG):
                     fn(jj, g)
-            kq = [bk[:2] for bk in cover if bk[2] == 1]
+            kq = [(bk[0], bk[1] // 2) for bk in cover if bk[1] % 2 == 1 and bk[2] == 1]
             if nxt and nxt[0] == "q":
-                for g in range(NG):
-                    if (nxt[1], g) in Q_ON_VECTOR:
-                        inter("V", "q", nxt[1], g)
-                        for u in kq:
-                            quant("k", *u)
-                        kq = []
-                    quant("q", nxt[1], g)
+                quant("q", nxt[1], 0)
+                inter("V", "q", nxt[1], 3)
+                for u in kq:
+                    quant("k", *u)
+                kq = []
+                quant("q", nxt[1], 1)
             for u in kq:
                 quant("k", *u)

@@ -25,7 +25,7 @@ NJ = E // NC
 NM = (B * S) // P
 HC = NC // HD
 
-Q_ON_VECTOR = ((0, 0), (0, 1), (0, 2), (0, 3), (1, 3), (2, 3), (3, 3))
+Q_ON_VECTOR = ((0, 0), (0, 1), (0, 2), (0, 3), (3, 3))
 COVER = (3, 3, 3, 3, 4, 0, 0, 0)
 VADD_COVERED = (3,)
 VADD_BARE = (2, 3)
@@ -39,7 +39,6 @@ def tile_llamaattention_pa_kernel(tc, x, Wq_bytes, Wq_scale, Wk, rope_cos, rope_
         raw = ctx.enter_context(tc.tile_pool(name="raw", bufs=12))
         work = ctx.enter_context(tc.tile_pool(name="work", bufs=3))
         psum = ctx.enter_context(tc.psum_pool(name="psum", bufs=4))
-        ctx.enter_context(tc.manual_schedule())
 
         wq_v = Wq_bytes.rearrange("(g p t) n -> g p t n", p=P, t=PACK)
         wk_v = Wk.rearrange("(g p t) n -> g p t n", p=P, t=PACK)
@@ -268,7 +267,8 @@ def tile_llamaattention_pa_kernel(tc, x, Wq_bytes, Wq_scale, Wk, rope_cos, rope_
             kq = [(bk[0], bk[1] // 2) for bk in cover if bk[1] % 2 == 1 and bk[2] == 1]
             if nxt and nxt[0] == "q":
                 quant("q", nxt[1], 0)
-                inter("V", "q", nxt[1], 3)
+                if (nxt[1], 3) in Q_ON_VECTOR:
+                    inter("V", "q", nxt[1], 3)
                 for u in kq:
                     quant("k", *u)
                 kq = []

@@ -27,8 +27,6 @@ HC = NC // HD
 
 Q_ON_VECTOR = ((0, 0), (0, 1), (0, 2), (0, 3), (3, 3))
 COVER = (3, 3, 3, 3, 4, 0, 0, 0)
-VADD_COVERED = (3,)
-VADD_BARE = (2, 3)
 
 
 def tile_llamaattention_pa_kernel(tc, x, Wq_bytes, Wq_scale, Wk, rope_cos, rope_sin, out_0, out_1):
@@ -69,7 +67,7 @@ def tile_llamaattention_pa_kernel(tc, x, Wq_bytes, Wq_scale, Wk, rope_cos, rope_
 
         def il_of(w, j, g):
             if (w, j, g // 2) not in il:
-                il[(w, j, g // 2)] = work.tile([P, 2, NC, PACK], BF16, name="il" + w, tag="il" + w, bufs=2, align_bytes=64)
+                il[(w, j, g // 2)] = work.tile([P, 2, NC, PACK], BF16, name="il" + w, tag="il" + w, bufs=(3 if w == "k" else 2), align_bytes=64)
             return il[(w, j, g // 2)]
 
         def inter(eng, w, j, g):
@@ -119,7 +117,7 @@ def tile_llamaattention_pa_kernel(tc, x, Wq_bytes, Wq_scale, Wk, rope_cos, rope_
 
         def products(w, j, m):
             shp = [P, 2, HC, HD]
-            t = work.tile(shp, F32, name="pab", tag="pab")
+            t = work.tile(shp, F32, name="pab", tag="pab", bufs=4)
             nc.vector.tensor_tensor(out=t[:], in0=tab[:, m % 2].unsqueeze(2).to_broadcast(shp),
                                     in1=acc[(w, j, m)][:].rearrange("p (h d) -> p h d", h=HC).unsqueeze(1).to_broadcast(shp),
                                     op=ALU.mult)
@@ -146,6 +144,8 @@ def tile_llamaattention_pa_kernel(tc, x, Wq_bytes, Wq_scale, Wk, rope_cos, rope_
         def ld_x(b):
             nc.sync.dma_start(out=x_sb[:, b, :, :], in_=x[b].rearrange("(p e) k -> p e k", e=2))
 
+        nc.scalar.dma_start(out=cos_sb[:], in_=rope_cos.rearrange("(p e) i -> p e i", e=2))
+        nc.scalar.dma_start(out=sin_sb[:], in_=rope_sin.rearrange("(p e) i -> p e i", e=2))
         nc.scalar.dma_start(out=scl[:], in_=Wq_scale.rearrange("(g p t) o -> p g (t o)", p=P, t=PACK))
         ld_k(0, 0)
         ld_q(0, 0)
@@ -157,8 +157,6 @@ def tile_llamaattention_pa_kernel(tc, x, Wq_bytes, Wq_scale, Wk, rope_cos, rope_
         ld_x(1)
         ld_k(0, 3)
         ld_q(0, 3)
-        nc.scalar.dma_start(out=cos_sb[:], in_=rope_cos.rearrange("(p e) i -> p e i", e=2))
-        nc.scalar.dma_start(out=sin_sb[:], in_=rope_sin.rearrange("(p e) i -> p e i", e=2))
         for j in (1, 2):
             for g in range(NG):
                 ld_k(j, g)
@@ -176,10 +174,10 @@ def tile_llamaattention_pa_kernel(tc, x, Wq_bytes, Wq_scale, Wk, rope_cos, rope_
         make_identity(nc, identb[:])
         tab = const.tile([P, 2, 2, HD], F32, name="tab")
         tabv = tab[:].rearrange("p e f (i r) -> p e f i r", r=2)
-        nc.gpsimd.tensor_copy(out=tabv[:, :, 0, :, 0], in_=cos_sb[:])
-        nc.gpsimd.tensor_copy(out=tabv[:, :, 0, :, 1], in_=cos_sb[:])
-        nc.gpsimd.tensor_copy(out=tabv[:, :, 1, :, 0], in_=sin_sb[:])
-        nc.gpsimd.tensor_scalar(out=tabv[:, :, 1, :, 1], in0=sin_sb[:], scalar1=-1.0, scalar2=None, op0=ALU.mult)
+        nc.vector.tensor_copy(out=tabv[:, :, 0, :, 0], in_=cos_sb[:])
+        nc.vector.tensor_copy(out=tabv[:, :, 0, :, 1], in_=cos_sb[:])
+        nc.vector.tensor_copy(out=tabv[:, :, 1, :, 0], in_=sin_sb[:])
+        nc.vector.tensor_scalar(out=tabv[:, :, 1, :, 1], in0=sin_sb[:], scalar1=-1.0, scalar2=None, op0=ALU.mult)
 
         xc = const.tile([P, B, NG, 2 * P], U32, name="xc", align_bytes=64)
         xs = const.tile([P, B, NG, 2 * P], U8, name="xs", align_bytes=64)
@@ -227,11 +225,10 @@ def tile_llamaattention_pa_kernel(tc, x, Wq_bytes, Wq_scale, Wk, rope_cos, rope_
             for h in range(2):
                 pe_inter(1, g, h)
                 empty("S", 1, g, h)
-        quant("k", 1, 0)
-        quant("k", 1, 1)
 
         seq = [(w, j) for j in range(NJ) for w in ("k", "q")]
         banks = [(j, g, h) for j in (2, 3) for g in range(NG) for h in range(2)]
+        ctx.enter_context(tc.manual_schedule(engines={mybir.EngineType.DVE, mybir.EngineType.Pool}))
         for i in range(len(seq)):
             w, j = seq[i]
             cover = banks[:COVER[i]]
@@ -240,38 +237,38 @@ def tile_llamaattention_pa_kernel(tc, x, Wq_bytes, Wq_scale, Wk, rope_cos, rope_
                 mm(w, j, m)
             for bk in cover:
                 pe_inter(*bk)
-            nxt = seq[i + 2] if i + 2 < len(seq) else None
-            if nxt and nxt[0] == "q":
-                for g in range(NG):
-                    widen(nxt[1], g)
-                    if (nxt[1], g) not in Q_ON_VECTOR:
-                        inter("S", "q", nxt[1], g)
-            vadd = VADD_COVERED if cover else VADD_BARE
+            js, hs = i // 2 + 1, i % 2
+            if js < NJ:
+                for g in (2 * hs, 2 * hs + 1):
+                    widen(js, g)
+                    if (js, g) not in Q_ON_VECTOR:
+                        inter("S", "q", js, g)
+            gadd = 3 if cover else 2
             for m in range(NM):
                 products(w, j, m)
-                if m not in vadd:
+                if m < gadd:
                     add(nc.gpsimd, w, j, m)
                     if m % 2 == 1:
                         store(w, j, m // 2)
             for bk in cover:
                 empty("V", *bk)
-            for m in vadd:
-                add(nc.vector, w, j, m)
-                if m % 2 == 1:
-                    store(w, j, m // 2)
             if late_loads:
                 fn, jj = late_loads[0]
                 late_loads = late_loads[1:]
                 for g in range(NG):
                     fn(jj, g)
-            kq = [(bk[0], bk[1] // 2) for bk in cover if bk[1] % 2 == 1 and bk[2] == 1]
-            if nxt and nxt[0] == "q":
-                quant("q", nxt[1], 0)
-                if (nxt[1], 3) in Q_ON_VECTOR:
-                    inter("V", "q", nxt[1], 3)
-                for u in kq:
-                    quant("k", *u)
-                kq = []
-                quant("q", nxt[1], 1)
-            for u in kq:
-                quant("k", *u)
+            jq, gq = (i + 1) // 2, (i - 1) % 2
+            if i >= 1 and jq < NJ:
+                if gq == 1 and (jq, 3) in Q_ON_VECTOR:
+                    inter("V", "q", jq, 3)
+                quant("q", jq, gq)
+            if i == 0:
+                quant("k", 1, 0)
+                quant("k", 1, 1)
+            for bk in cover:
+                if bk[1] % 2 == 1 and bk[2] == 1:
+                    quant("k", bk[0], bk[1] // 2)
+            for m in range(gadd, NM):
+                add(nc.vector, w, j, m)
+                if m % 2 == 1:
+                    store(w, j, m // 2)

@@ -71,12 +71,12 @@ def tile_llamaattention_pa_kernel(tc, x, Wq_bytes, Wq_scale, Wk, rope_cos, rope_
             return il[(w, j, g // 2)]
 
         def inter(eng, w, j, g):
-            t = il_of(w, j, g)
-            view = src[(w, j, g)][:].rearrange("p t c -> p c t")
+            dst = il_of(w, j, g)[:, g % 2].rearrange("p (c i) t -> p c t i", i=4)
+            view = src[(w, j, g)][:].rearrange("p t (c i) -> p c t i", i=4)
             if eng == "V":
-                nc.vector.tensor_copy(out=t[:, g % 2], in_=view)
+                nc.vector.tensor_copy(out=dst, in_=view)
             else:
-                nc.scalar.copy(out=t[:, g % 2], in_=view)
+                nc.scalar.copy(out=dst, in_=view)
 
         def pe_inter(j, g, h):
             t = psum.tile([P, NC // 2, PACK], BF16, name="stg", tag="stg")

@@ -25,8 +25,8 @@ NJ = E // NC
 NM = (B * S) // P
 HC = NC // HD
 
-Q_ON_VECTOR = ((0, 0), (0, 1), (0, 2), (0, 3), (3, 3))
-COVER = (3, 3, 3, 3, 4, 0, 0, 0)
+Q_ON_VECTOR = ((0, 0), (0, 1), (0, 2), (0, 3), (1, 1), (1, 3), (2, 1), (2, 3), (3, 1), (3, 3))
+COVER = (4, 4, 4, 4, 0, 0, 0, 0)
 
 
 def tile_llamaattention_pa_kernel(tc, x, Wq_bytes, Wq_scale, Wk, rope_cos, rope_sin, out_0, out_1):
@@ -229,29 +229,29 @@ def tile_llamaattention_pa_kernel(tc, x, Wq_bytes, Wq_scale, Wk, rope_cos, rope_
         seq = [(w, j) for j in range(NJ) for w in ("k", "q")]
         banks = [(j, g, h) for j in (2, 3) for g in range(NG) for h in range(2)]
         ctx.enter_context(tc.manual_schedule(engines={mybir.EngineType.DVE, mybir.EngineType.Pool}))
+        done = []
         for i in range(len(seq)):
             w, j = seq[i]
             cover = banks[:COVER[i]]
             banks = banks[COVER[i]:]
             for m in range(NM):
                 mm(w, j, m)
-            for bk in cover:
-                pe_inter(*bk)
             js, hs = i // 2 + 1, i % 2
             if js < NJ:
                 for g in (2 * hs, 2 * hs + 1):
                     widen(js, g)
                     if (js, g) not in Q_ON_VECTOR:
                         inter("S", "q", js, g)
-            gadd = 3 if cover else 2
+            for bk in cover:
+                pe_inter(*bk)
+                empty("S", *bk)
+            gadd = 3 if i < 5 else 2
             for m in range(NM):
                 products(w, j, m)
                 if m < gadd:
                     add(nc.gpsimd, w, j, m)
                     if m % 2 == 1:
                         store(w, j, m // 2)
-            for bk in cover:
-                empty("V", *bk)
             if late_loads:
                 fn, jj = late_loads[0]
                 late_loads = late_loads[1:]
@@ -259,15 +259,16 @@ def tile_llamaattention_pa_kernel(tc, x, Wq_bytes, Wq_scale, Wk, rope_cos, rope_
                     fn(jj, g)
             jq, gq = (i + 1) // 2, (i - 1) % 2
             if i >= 1 and jq < NJ:
-                if gq == 1 and (jq, 3) in Q_ON_VECTOR:
-                    inter("V", "q", jq, 3)
+                for g in (2 * gq, 2 * gq + 1):
+                    if (jq, g) in Q_ON_VECTOR:
+                        inter("V", "q", jq, g)
                 quant("q", jq, gq)
             if i == 0:
                 quant("k", 1, 0)
                 quant("k", 1, 1)
-            for bk in cover:
-                if bk[1] % 2 == 1 and bk[2] == 1:
-                    quant("k", bk[0], bk[1] // 2)
+            for u in done:
+                quant("k", *u)
+            done = [(cover[0][0], cover[0][1] // 2)] if cover else []
             for m in range(gadd, NM):
                 add(nc.vector, w, j, m)
                 if m % 2 == 1:

@@ -25,7 +25,7 @@ NJ = E // NC
 NM = (B * S) // P
 HC = NC // HD
 
-Q_ON_VECTOR = ((0, 0), (0, 1), (0, 2), (0, 3), (1, 1), (1, 3), (2, 1), (2, 3), (3, 1), (3, 3))
+Q_ON_VECTOR = ((0, 0), (0, 1), (0, 2), (0, 3), (1, 3), (2, 3), (3, 3))
 COVER = (4, 4, 4, 4, 0, 0, 0, 0)
 
 
@@ -88,11 +88,12 @@ def tile_llamaattention_pa_kernel(tc, x, Wq_bytes, Wq_scale, Wk, rope_cos, rope_
             stage[(j, g, h)] = t
 
         def empty(eng, j, g, h):
-            dst = il_of("k", j, g)[:, g % 2, h * 256:(h + 1) * 256, :]
+            dst = il_of("k", j, g)[:, g % 2, h * 256:(h + 1) * 256, :].rearrange("p c t -> p (c t)").bitcast(F32)
+            words = stage[(j, g, h)][:].rearrange("p c t -> p (c t)").bitcast(F32)
             if eng == "V":
-                nc.vector.tensor_copy(out=dst, in_=stage[(j, g, h)][:])
+                nc.vector.tensor_copy(out=dst, in_=words)
             else:
-                nc.scalar.copy(out=dst, in_=stage[(j, g, h)][:])
+                nc.scalar.copy(out=dst, in_=words)
 
         def quant(w, j, gg):
             if gg == 0:
@@ -104,16 +105,17 @@ def tile_llamaattention_pa_kernel(tc, x, Wq_bytes, Wq_scale, Wk, rope_cos, rope_
                                   scales=s[:, 2 * gg:2 * gg + 2, :].rearrange("p g c -> p (g c)"),
                                   in_=il[(w, j, gg)][:].rearrange("p g c t -> p (g c t)"))
 
-        def mm(w, j, m):
-            t = psum.tile([P, NC], F32, name="acc", tag="acc")
+        def mm(w, j, m, gs):
+            if gs[0] == 0:
+                acc[(w, j, m)] = psum.tile([P, NC], F32, name="acc", tag="acc")
+            t = acc[(w, j, m)]
             c, s = codes[(w, j)]
             b, e = m // 2, m % 2
-            for g in range(NG):
+            for g in gs:
                 nc.tensor.matmul_mx(out=t[:], lhsT=xc[:, b, g, e * P:(e + 1) * P].bitcast(FP8X4),
                                     lhsT_scale=xs[:, b, g, e * P:(e + 1) * P],
                                     rhs=c[:, g, :].bitcast(FP8X4), rhs_scale=s[:, g, :],
                                     start=(g == 0), stop=(g == NG - 1))
-            acc[(w, j, m)] = t
 
         def products(w, j, m):
             shp = [P, 2, HC, HD]
@@ -123,18 +125,18 @@ def tile_llamaattention_pa_kernel(tc, x, Wq_bytes, Wq_scale, Wk, rope_cos, rope_
                                     op=ALU.mult)
             prod[(w, j, m)] = t
 
-        def add(eng, w, j, m):
+        def add(eng, w, j, m, h0=0, h1=HC):
             b, e = m // 2, m % 2
             if e == 0:
                 res[(w, j, b)] = work.tile([P, HC, 2, HD], F32, name="r", tag="r")
             t = prod[(w, j, m)]
-            eng.tensor_tensor(out=res[(w, j, b)][:, :, e, :].rearrange("p h (i r) -> p h i r", r=2),
-                              in0=t[:, 0].rearrange("p h (i r) -> p h i r", r=2),
-                              in1=t[:, 1].rearrange("p h (i r) -> p h i r", r=2)[:, :, :, ::-1], op=ALU.add)
+            eng.tensor_tensor(out=res[(w, j, b)][:, h0:h1, e, :].rearrange("p h (i r) -> p h i r", r=2),
+                              in0=t[:, 0, h0:h1].rearrange("p h (i r) -> p h i r", r=2),
+                              in1=t[:, 1, h0:h1].rearrange("p h (i r) -> p h i r", r=2)[:, :, :, ::-1], op=ALU.add)
 
-        def store(w, j, b):
-            nc.sync.dma_start(out=outs[w][b, j * HC:(j + 1) * HC].rearrange("h (p e) d -> p h (e d)", e=2),
-                              in_=res[(w, j, b)][:].rearrange("p h e d -> p h (e d)"))
+        def store(w, j, b, h0=0, h1=HC):
+            nc.sync.dma_start(out=outs[w][b, j * HC + h0:j * HC + h1].rearrange("h (p e) d -> p h (e d)", e=2),
+                              in_=res[(w, j, b)][:, h0:h1].rearrange("p h e d -> p h (e d)"))
 
         scl = const.tile([P, NG, PACK], F32, name="scl")
         x_sb = const.tile([P, B, 2, D], BF16, name="x_sb")
@@ -144,11 +146,11 @@ def tile_llamaattention_pa_kernel(tc, x, Wq_bytes, Wq_scale, Wk, rope_cos, rope_
         def ld_x(b):
             nc.sync.dma_start(out=x_sb[:, b, :, :], in_=x[b].rearrange("(p e) k -> p e k", e=2))
 
+        nc.scalar.dma_start(out=scl[:], in_=Wq_scale.rearrange("(g p t) o -> p g (t o)", p=P, t=PACK))
         nc.scalar.dma_start(out=cos_sb[:], in_=rope_cos.rearrange("(p e) i -> p e i", e=2))
         nc.scalar.dma_start(out=sin_sb[:], in_=rope_sin.rearrange("(p e) i -> p e i", e=2))
-        nc.scalar.dma_start(out=scl[:], in_=Wq_scale.rearrange("(g p t) o -> p g (t o)", p=P, t=PACK))
-        ld_k(0, 0)
         ld_q(0, 0)
+        ld_k(0, 0)
         ld_q(0, 1)
         ld_k(0, 1)
         ld_x(0)
@@ -234,12 +236,14 @@ def tile_llamaattention_pa_kernel(tc, x, Wq_bytes, Wq_scale, Wk, rope_cos, rope_
             w, j = seq[i]
             cover = banks[:COVER[i]]
             banks = banks[COVER[i]:]
-            for m in range(NM):
-                mm(w, j, m)
+            for gs in ((0, 1), (2, 3)):
+                for m in range(NM):
+                    mm(w, j, m, gs)
             js, hs = i // 2 + 1, i % 2
             if js < NJ:
-                for g in (2 * hs, 2 * hs + 1):
+                for g in (2 * hs + 1, 2 * hs):
                     widen(js, g)
+                for g in (2 * hs, 2 * hs + 1):
                     if (js, g) not in Q_ON_VECTOR:
                         inter("S", "q", js, g)
             for bk in cover:
@@ -257,6 +261,12 @@ def tile_llamaattention_pa_kernel(tc, x, Wq_bytes, Wq_scale, Wk, rope_cos, rope_
                 late_loads = late_loads[1:]
                 for g in range(NG):
                     fn(jj, g)
+            early = i == len(seq) - 2
+            if early:
+                for m in range(gadd, NM):
+                    add(nc.vector, w, j, m)
+                    if m % 2 == 1:
+                        store(w, j, m // 2)
             jq, gq = (i + 1) // 2, (i - 1) % 2
             if i >= 1 and jq < NJ:
                 for g in (2 * gq, 2 * gq + 1):
@@ -270,6 +280,13 @@ def tile_llamaattention_pa_kernel(tc, x, Wq_bytes, Wq_scale, Wk, rope_cos, rope_
                 quant("k", *u)
             done = [(cover[0][0], cover[0][1] // 2)] if cover else []
             for m in range(gadd, NM):
-                add(nc.vector, w, j, m)
-                if m % 2 == 1:
-                    store(w, j, m // 2)
+                if early:
+                    continue
+                if i == len(seq) - 1 and m == NM - 1:
+                    for h0 in (0, HC // 2):
+                        add(nc.vector, w, j, m, h0, h0 + HC // 2)
+                        store(w, j, m // 2, h0, h0 + HC // 2)
+                else:
+                    add(nc.vector, w, j, m)
+                    if m % 2 == 1:
+                        store(w, j, m // 2)

@@ -49,7 +49,7 @@ def tile_llamaattention_pa_kernel(tc, x, Wq_bytes, Wq_scale, Wk, rope_cos, rope_
         res = {}
 
         def ld_q(j, g):
-            t = raw.tile([P, PACK, NC], U8, name="qbytes", tag="qbytes")
+            t = raw.tile([P, PACK, NC], U8, name="qbytes", tag="qbytes", bufs=10)
             nc.sync.dma_start(out=t[:], in_=wq_v[g, :, :, j * NC:(j + 1) * NC])
             src[("b", j, g)] = t
 
@@ -119,7 +119,7 @@ def tile_llamaattention_pa_kernel(tc, x, Wq_bytes, Wq_scale, Wk, rope_cos, rope_
 
         def products(w, j, m):
             shp = [P, 2, HC, HD]
-            t = work.tile(shp, F32, name="pab", tag="pab", bufs=4)
+            t = work.tile(shp, F32, name="pab", tag="pab", bufs=5)
             nc.vector.tensor_tensor(out=t[:], in0=tab[:, m % 2].unsqueeze(2).to_broadcast(shp),
                                     in1=acc[(w, j, m)][:].rearrange("p (h d) -> p h d", h=HC).unsqueeze(1).to_broadcast(shp),
                                     op=ALU.mult)
@@ -127,7 +127,7 @@ def tile_llamaattention_pa_kernel(tc, x, Wq_bytes, Wq_scale, Wk, rope_cos, rope_
 
         def add(eng, w, j, m, h0=0, h1=HC):
             b, e = m // 2, m % 2
-            if e == 0:
+            if (w, j, b) not in res:
                 res[(w, j, b)] = work.tile([P, HC, 2, HD], F32, name="r", tag="r")
             t = prod[(w, j, m)]
             eng.tensor_tensor(out=res[(w, j, b)][:, h0:h1, e, :].rearrange("p h (i r) -> p h i r", r=2),
@@ -137,6 +137,16 @@ def tile_llamaattention_pa_kernel(tc, x, Wq_bytes, Wq_scale, Wk, rope_cos, rope_
         def store(w, j, b, h0=0, h1=HC):
             nc.sync.dma_start(out=outs[w][b, j * HC + h0:j * HC + h1].rearrange("h (p e) d -> p h (e d)", e=2),
                               in_=res[(w, j, b)][:, h0:h1].rearrange("p h e d -> p h (e d)"))
+
+        sink = const.tile([P, 1], F32, name="sink")
+        flags = {}
+
+        def raise_flag(i):
+            flags[i] = work.tile([P, 1], F32, name="flag", tag="flag", bufs=2)
+            nc.vector.memset(flags[i][:], 0.0)
+
+        def await_flag(i):
+            nc.gpsimd.tensor_copy(out=sink[:], in_=flags[i][:])
 
         scl = const.tile([P, NG, PACK], F32, name="scl")
         x_sb = const.tile([P, B, 2, D], BF16, name="x_sb")
@@ -232,6 +242,7 @@ def tile_llamaattention_pa_kernel(tc, x, Wq_bytes, Wq_scale, Wk, rope_cos, rope_
         banks = [(j, g, h) for j in (2, 3) for g in range(NG) for h in range(2)]
         ctx.enter_context(tc.manual_schedule(engines={mybir.EngineType.DVE, mybir.EngineType.Pool}))
         done = []
+        held = None
         for i in range(len(seq)):
             w, j = seq[i]
             cover = banks[:COVER[i]]
@@ -249,7 +260,14 @@ def tile_llamaattention_pa_kernel(tc, x, Wq_bytes, Wq_scale, Wk, rope_cos, rope_
             for bk in cover:
                 pe_inter(*bk)
                 empty("S", *bk)
-            gadd = 3 if i < 5 else 2
+            gadd = 2
+            if held:
+                await_flag(i - 1)
+                add(nc.gpsimd, held[0], held[1], 2)
+                store(held[0], held[1], 1)
+            last = i == len(seq) - 1
+            held = None if last else (w, j)
+            vadds = (2, 3) if last else (3,)
             for m in range(NM):
                 products(w, j, m)
                 if m < gadd:
@@ -263,15 +281,15 @@ def tile_llamaattention_pa_kernel(tc, x, Wq_bytes, Wq_scale, Wk, rope_cos, rope_
                     fn(jj, g)
             early = i == len(seq) - 2
             if early:
-                for m in range(gadd, NM):
+                for m in vadds:
                     add(nc.vector, w, j, m)
-                    if m % 2 == 1:
-                        store(w, j, m // 2)
             jq, gq = (i + 1) // 2, (i - 1) % 2
             if i >= 1 and jq < NJ:
                 for g in (2 * gq, 2 * gq + 1):
                     if (jq, g) in Q_ON_VECTOR:
                         inter("V", "q", jq, g)
+                if early:
+                    raise_flag(i)
                 quant("q", jq, gq)
             if i == 0:
                 quant("k", 1, 0)
@@ -279,14 +297,14 @@ def tile_llamaattention_pa_kernel(tc, x, Wq_bytes, Wq_scale, Wk, rope_cos, rope_
             for u in done:
                 quant("k", *u)
             done = [(cover[0][0], cover[0][1] // 2)] if cover else []
-            for m in range(gadd, NM):
+            for m in vadds:
                 if early:
                     continue
-                if i == len(seq) - 1 and m == NM - 1:
+                if last and m == NM - 1:
                     for h0 in (0, HC // 2):
                         add(nc.vector, w, j, m, h0, h0 + HC // 2)
                         store(w, j, m // 2, h0, h0 + HC // 2)
                 else:
+                    if not last:
+                        raise_flag(i)
                     add(nc.vector, w, j, m)
-                    if m % 2 == 1:
-                        store(w, j, m // 2)

@@ -49,7 +49,7 @@ def tile_llamaattention_pa_kernel(tc, x, Wq_bytes, Wq_scale, Wk, rope_cos, rope_
         res = {}
 
         def ld_q(j, g):
-            t = raw.tile([P, PACK, NC], U8, name="qbytes", tag="qbytes", bufs=10)
+            t = raw.tile([P, PACK, NC], U8, name="qbytes", tag="qbytes", bufs=8)
             nc.sync.dma_start(out=t[:], in_=wq_v[g, :, :, j * NC:(j + 1) * NC])
             src[("b", j, g)] = t
 
@@ -119,7 +119,7 @@ def tile_llamaattention_pa_kernel(tc, x, Wq_bytes, Wq_scale, Wk, rope_cos, rope_
 
         def products(w, j, m):
             shp = [P, 2, HC, HD]
-            t = work.tile(shp, F32, name="pab", tag="pab", bufs=5)
+            t = work.tile(shp, F32, name="pab", tag="pab", bufs=6)
             nc.vector.tensor_tensor(out=t[:], in0=tab[:, m % 2].unsqueeze(2).to_broadcast(shp),
                                     in1=acc[(w, j, m)][:].rearrange("p (h d) -> p h d", h=HC).unsqueeze(1).to_broadcast(shp),
                                     op=ALU.mult)
@@ -264,10 +264,11 @@ def tile_llamaattention_pa_kernel(tc, x, Wq_bytes, Wq_scale, Wk, rope_cos, rope_
             if held:
                 await_flag(i - 1)
                 add(nc.gpsimd, held[0], held[1], 2)
+                add(nc.gpsimd, held[0], held[1], 3)
                 store(held[0], held[1], 1)
             last = i == len(seq) - 1
             held = None if last else (w, j)
-            vadds = (2, 3) if last else (3,)
+            vadds = (2, 3) if last else ()
             for m in range(NM):
                 products(w, j, m)
                 if m < gadd:
@@ -279,32 +280,30 @@ def tile_llamaattention_pa_kernel(tc, x, Wq_bytes, Wq_scale, Wk, rope_cos, rope_
                 late_loads = late_loads[1:]
                 for g in range(NG):
                     fn(jj, g)
-            early = i == len(seq) - 2
-            if early:
-                for m in vadds:
-                    add(nc.vector, w, j, m)
             jq, gq = (i + 1) // 2, (i - 1) % 2
+            post = []
             if i >= 1 and jq < NJ:
                 for g in (2 * gq, 2 * gq + 1):
                     if (jq, g) in Q_ON_VECTOR:
-                        inter("V", "q", jq, g)
-                if early:
-                    raise_flag(i)
-                quant("q", jq, gq)
+                        post.append(("inter", "q", jq, g))
+                post.append(("quant", "q", jq, gq))
             if i == 0:
-                quant("k", 1, 0)
-                quant("k", 1, 1)
+                post.append(("quant", "k", 1, 0))
+                post.append(("quant", "k", 1, 1))
             for u in done:
-                quant("k", *u)
+                post.append(("quant", "k", u[0], u[1]))
             done = [(cover[0][0], cover[0][1] // 2)] if cover else []
+            for n in range(len(post)):
+                if n == len(post) - 1:
+                    raise_flag(i)
+                if post[n][0] == "inter":
+                    inter("V", post[n][1], post[n][2], post[n][3])
+                else:
+                    quant(post[n][1], post[n][2], post[n][3])
             for m in vadds:
-                if early:
-                    continue
-                if last and m == NM - 1:
+                if m == NM - 1:
                     for h0 in (0, HC // 2):
                         add(nc.vector, w, j, m, h0, h0 + HC // 2)
                         store(w, j, m // 2, h0, h0 + HC // 2)
                 else:
-                    if not last:
-                        raise_flag(i)
                     add(nc.vector, w, j, m)

@@ -26,7 +26,7 @@ NM = (B * S) // P
 HC = NC // HD
 
 Q_ON_VECTOR = ((0, 0), (0, 1), (0, 2), (0, 3), (1, 3), (2, 3), (3, 3))
-COVER = (4, 4, 4, 4, 0, 0, 0, 0)
+COVER = (0, 4, 4, 4, 4, 0, 0, 0)
 
 
 def tile_llamaattention_pa_kernel(tc, x, Wq_bytes, Wq_scale, Wk, rope_cos, rope_sin, out_0, out_1):
@@ -47,6 +47,7 @@ def tile_llamaattention_pa_kernel(tc, x, Wq_bytes, Wq_scale, Wk, rope_cos, rope_
         acc = {}
         prod = {}
         res = {}
+        ready = []
 
         def ld_q(j, g):
             t = raw.tile([P, PACK, NC], U8, name="qbytes", tag="qbytes", bufs=8)
@@ -101,6 +102,7 @@ def tile_llamaattention_pa_kernel(tc, x, Wq_bytes, Wq_scale, Wk, rope_cos, rope_
                 s = work.tile([P, NG, NC], U8, name=w + "s", tag=w + "s", bufs=2, align_bytes=64)
                 codes[(w, j)] = (c, s)
             c, s = codes[(w, j)]
+            ready.append((w, j, gg))
             nc.vector.quantize_mx(out=c[:, 2 * gg:2 * gg + 2, :].rearrange("p g c -> p (g c)").bitcast(FP8X4),
                                   scales=s[:, 2 * gg:2 * gg + 2, :].rearrange("p g c -> p (g c)"),
                                   in_=il[(w, j, gg)][:].rearrange("p g c t -> p (g c t)"))
@@ -240,16 +242,19 @@ def tile_llamaattention_pa_kernel(tc, x, Wq_bytes, Wq_scale, Wk, rope_cos, rope_
 
         seq = [(w, j) for j in range(NJ) for w in ("k", "q")]
         banks = [(j, g, h) for j in (2, 3) for g in range(NG) for h in range(2)]
-        ctx.enter_context(tc.manual_schedule(engines={mybir.EngineType.DVE, mybir.EngineType.Pool}))
-        done = []
+        ctx.enter_context(tc.manual_schedule(engines={mybir.EngineType.DVE, mybir.EngineType.Pool, mybir.EngineType.PE}))
+        for gs in ((0, 1), (2, 3)):
+            for m in range(NM):
+                mm("k", 0, m, gs)
+        filled = []
         held = None
         for i in range(len(seq)):
             w, j = seq[i]
+            last = i == len(seq) - 1
+            nxt = None if last else seq[i + 1]
+            whole = (not last) and (nxt[0], nxt[1], 1) in ready
             cover = banks[:COVER[i]]
             banks = banks[COVER[i]:]
-            for gs in ((0, 1), (2, 3)):
-                for m in range(NM):
-                    mm(w, j, m, gs)
             js, hs = i // 2 + 1, i % 2
             if js < NJ:
                 for g in (2 * hs + 1, 2 * hs):
@@ -257,24 +262,25 @@ def tile_llamaattention_pa_kernel(tc, x, Wq_bytes, Wq_scale, Wk, rope_cos, rope_
                 for g in (2 * hs, 2 * hs + 1):
                     if (js, g) not in Q_ON_VECTOR:
                         inter("S", "q", js, g)
-            for bk in cover:
-                pe_inter(*bk)
-                empty("S", *bk)
-            gadd = 2
             if held:
                 await_flag(i - 1)
                 add(nc.gpsimd, held[0], held[1], 2)
                 add(nc.gpsimd, held[0], held[1], 3)
                 store(held[0], held[1], 1)
-            last = i == len(seq) - 1
             held = None if last else (w, j)
-            vadds = (2, 3) if last else ()
             for m in range(NM):
                 products(w, j, m)
-                if m < gadd:
+                if m < 2:
                     add(nc.gpsimd, w, j, m)
-                    if m % 2 == 1:
-                        store(w, j, m // 2)
+                    if m == 1:
+                        store(w, j, 0)
+                if m < len(cover):
+                    pe_inter(*cover[m])
+                    empty("S", *cover[m])
+                if nxt:
+                    mm(nxt[0], nxt[1], m, (0, 1))
+                    if whole:
+                        mm(nxt[0], nxt[1], m, (2, 3))
             if late_loads:
                 fn, jj = late_loads[0]
                 late_loads = late_loads[1:]
@@ -290,9 +296,12 @@ def tile_llamaattention_pa_kernel(tc, x, Wq_bytes, Wq_scale, Wk, rope_cos, rope_
             if i == 0:
                 post.append(("quant", "k", 1, 0))
                 post.append(("quant", "k", 1, 1))
-            for u in done:
-                post.append(("quant", "k", u[0], u[1]))
-            done = [(cover[0][0], cover[0][1] // 2)] if cover else []
+            for u in filled:
+                if nxt and nxt[0] == "k":
+                    post = [("quant", "k", u[0], u[1])] + post
+                else:
+                    post.append(("quant", "k", u[0], u[1]))
+            filled = [(cover[0][0], cover[0][1] // 2)] if cover else []
             for n in range(len(post)):
                 if n == len(post) - 1:
                     raise_flag(i)
@@ -300,10 +309,11 @@ def tile_llamaattention_pa_kernel(tc, x, Wq_bytes, Wq_scale, Wk, rope_cos, rope_
                     inter("V", post[n][1], post[n][2], post[n][3])
                 else:
                     quant(post[n][1], post[n][2], post[n][3])
-            for m in vadds:
-                if m == NM - 1:
-                    for h0 in (0, HC // 2):
-                        add(nc.vector, w, j, m, h0, h0 + HC // 2)
-                        store(w, j, m // 2, h0, h0 + HC // 2)
-                else:
-                    add(nc.vector, w, j, m)
+            if nxt and not whole:
+                for m in range(NM):
+                    mm(nxt[0], nxt[1], m, (2, 3))
+            if last:
+                add(nc.vector, w, j, 2)
+                for h0 in (0, HC // 2):
+                    add(nc.vector, w, j, 3, h0, h0 + HC // 2)
+                    store(w, j, 1, h0, h0 + HC // 2)

@@ -25,7 +25,7 @@ NJ = E // NC
 NM = (B * S) // P
 HC = NC // HD
 
-Q_ON_VECTOR = ((0, 0), (0, 1), (0, 2), (0, 3), (1, 3), (2, 3), (3, 3))
+Q_ON_VECTOR = ((0, 0), (0, 1), (0, 2), (0, 3), (1, 3), (2, 1), (2, 3), (3, 3))
 COVER = (0, 4, 4, 4, 4, 0, 0, 0)
 
 
@@ -96,18 +96,28 @@ def tile_llamaattention_pa_kernel(tc, x, Wq_bytes, Wq_scale, Wk, rope_cos, rope_
             else:
                 nc.scalar.copy(out=dst, in_=words)
 
-        def quant(w, j, gg):
-            if gg == 0:
+        def codes_of(w, j):
+            if (w, j) not in codes:
                 c = work.tile([P, NG, NC], U32, name=w + "c", tag=w + "c", bufs=2, align_bytes=64)
                 s = work.tile([P, NG, NC], U8, name=w + "s", tag=w + "s", bufs=2, align_bytes=64)
                 codes[(w, j)] = (c, s)
-            c, s = codes[(w, j)]
-            ready.append((w, j, gg))
+            return codes[(w, j)]
+
+        def quant_unit(w, j, g):
+            c, s = codes_of(w, j)
+            ready.append((w, j, g))
+            nc.vector.quantize_mx(out=c[:, g, :].bitcast(FP8X4), scales=s[:, g, :],
+                                  in_=il[(w, j, g // 2)][:, g % 2].rearrange("p c t -> p (c t)"))
+
+        def quant(w, j, gg):
+            c, s = codes_of(w, j)
+            ready.append((w, j, 2 * gg))
+            ready.append((w, j, 2 * gg + 1))
             nc.vector.quantize_mx(out=c[:, 2 * gg:2 * gg + 2, :].rearrange("p g c -> p (g c)").bitcast(FP8X4),
                                   scales=s[:, 2 * gg:2 * gg + 2, :].rearrange("p g c -> p (g c)"),
                                   in_=il[(w, j, gg)][:].rearrange("p g c t -> p (g c t)"))
 
-        def mm(w, j, m, gs):
+        def mm(w, j, m, gs, closes):
             if gs[0] == 0:
                 acc[(w, j, m)] = psum.tile([P, NC], F32, name="acc", tag="acc")
             t = acc[(w, j, m)]
@@ -117,7 +127,7 @@ def tile_llamaattention_pa_kernel(tc, x, Wq_bytes, Wq_scale, Wk, rope_cos, rope_
                 nc.tensor.matmul_mx(out=t[:], lhsT=xc[:, b, g, e * P:(e + 1) * P].bitcast(FP8X4),
                                     lhsT_scale=xs[:, b, g, e * P:(e + 1) * P],
                                     rhs=c[:, g, :].bitcast(FP8X4), rhs_scale=s[:, g, :],
-                                    start=(g == 0), stop=(g == NG - 1))
+                                    start=(g == 0), stop=(closes and g == gs[-1]))
 
         def products(w, j, m):
             shp = [P, 2, HC, HD]
@@ -213,28 +223,29 @@ def tile_llamaattention_pa_kernel(tc, x, Wq_bytes, Wq_scale, Wk, rope_cos, rope_
                                   scales=xs[:, b].rearrange("p g c -> p (g c)"),
                                   in_=xg[b][:].rearrange("p g c -> p (g c)"))
 
-        widen(0, 0)
-        widen(0, 1)
-        inter("V", "k", 0, 0)
-        inter("V", "q", 0, 0)
-        inter("V", "k", 0, 1)
-        inter("V", "q", 0, 1)
-        quant("k", 0, 0)
-        quant("q", 0, 0)
-        for g in range(NG):
-            x_turn(0, g)
-        widen(0, 2)
-        inter("V", "k", 0, 2)
-        x_quant(0)
-        inter("V", "q", 0, 2)
-        for g in range(NG):
-            x_turn(1, g)
-        widen(0, 3)
-        inter("V", "k", 0, 3)
-        inter("V", "q", 0, 3)
-        quant("k", 0, 1)
-        x_quant(1)
-        quant("q", 0, 1)
+        with tc.manual_schedule(engines={mybir.EngineType.DVE}):
+            widen(0, 0)
+            widen(0, 1)
+            inter("V", "k", 0, 0)
+            inter("V", "q", 0, 0)
+            inter("V", "k", 0, 1)
+            inter("V", "q", 0, 1)
+            quant("k", 0, 0)
+            quant("q", 0, 0)
+            for g in range(NG):
+                x_turn(0, g)
+            widen(0, 2)
+            inter("V", "k", 0, 2)
+            x_quant(0)
+            inter("V", "q", 0, 2)
+            for g in range(NG):
+                x_turn(1, g)
+            widen(0, 3)
+            inter("V", "k", 0, 3)
+            quant("k", 0, 1)
+            x_quant(1)
+            inter("V", "q", 0, 3)
+            quant("q", 0, 1)
         for g in range(NG):
             for h in range(2):
                 pe_inter(1, g, h)
@@ -243,16 +254,18 @@ def tile_llamaattention_pa_kernel(tc, x, Wq_bytes, Wq_scale, Wk, rope_cos, rope_
         seq = [(w, j) for j in range(NJ) for w in ("k", "q")]
         banks = [(j, g, h) for j in (2, 3) for g in range(NG) for h in range(2)]
         ctx.enter_context(tc.manual_schedule(engines={mybir.EngineType.DVE, mybir.EngineType.Pool, mybir.EngineType.PE}))
-        for gs in ((0, 1), (2, 3)):
-            for m in range(NM):
-                mm("k", 0, m, gs)
+        for m in range(NM):
+            mm("k", 0, m, (0, 1), False)
+        for m in range(NM):
+            mm("k", 0, m, (2, 3), True)
         filled = []
         held = None
         for i in range(len(seq)):
             w, j = seq[i]
             last = i == len(seq) - 1
             nxt = None if last else seq[i + 1]
-            whole = (not last) and (nxt[0], nxt[1], 1) in ready
+            early = () if last else tuple([g for g in range(NG) if (nxt[0], nxt[1], g) in ready])
+            late = () if last else tuple([g for g in reversed(range(NG)) if g not in early])
             cover = banks[:COVER[i]]
             banks = banks[COVER[i]:]
             js, hs = i // 2 + 1, i % 2
@@ -278,9 +291,7 @@ def tile_llamaattention_pa_kernel(tc, x, Wq_bytes, Wq_scale, Wk, rope_cos, rope_
                     pe_inter(*cover[m])
                     empty("S", *cover[m])
                 if nxt:
-                    mm(nxt[0], nxt[1], m, (0, 1))
-                    if whole:
-                        mm(nxt[0], nxt[1], m, (2, 3))
+                    mm(nxt[0], nxt[1], m, early, not late)
             if late_loads:
                 fn, jj = late_loads[0]
                 late_loads = late_loads[1:]
@@ -292,26 +303,33 @@ def tile_llamaattention_pa_kernel(tc, x, Wq_bytes, Wq_scale, Wk, rope_cos, rope_
                 for g in (2 * gq, 2 * gq + 1):
                     if (jq, g) in Q_ON_VECTOR:
                         post.append(("inter", "q", jq, g))
-                post.append(("quant", "q", jq, gq))
+                if i == len(seq) - 2:
+                    post.append(("unit", "q", jq, 3))
+                    post.append(("unit", "q", jq, 2))
+                else:
+                    post.append(("half", "q", jq, gq))
             if i == 0:
-                post.append(("quant", "k", 1, 0))
-                post.append(("quant", "k", 1, 1))
+                post.append(("half", "k", 1, 0))
+                post.append(("half", "k", 1, 1))
             for u in filled:
                 if nxt and nxt[0] == "k":
-                    post = [("quant", "k", u[0], u[1])] + post
+                    post = [("half", "k", u[0], u[1])] + post
                 else:
-                    post.append(("quant", "k", u[0], u[1]))
+                    post.append(("half", "k", u[0], u[1]))
             filled = [(cover[0][0], cover[0][1] // 2)] if cover else []
             for n in range(len(post)):
+                kind, a, b, c = post[n]
                 if n == len(post) - 1:
                     raise_flag(i)
-                if post[n][0] == "inter":
-                    inter("V", post[n][1], post[n][2], post[n][3])
+                if kind == "inter":
+                    inter("V", a, b, c)
+                elif kind == "half":
+                    quant(a, b, c)
                 else:
-                    quant(post[n][1], post[n][2], post[n][3])
-            if nxt and not whole:
+                    quant_unit(a, b, c)
+            if late:
                 for m in range(NM):
-                    mm(nxt[0], nxt[1], m, (2, 3))
+                    mm(nxt[0], nxt[1], m, late, True)
             if last:
                 add(nc.vector, w, j, 2)
                 for h0 in (0, HC // 2):

@@ -253,7 +253,7 @@ def tile_llamaattention_pa_kernel(tc, x, Wq_bytes, Wq_scale, Wk, rope_cos, rope_
 
         seq = [(w, j) for j in range(NJ) for w in ("k", "q")]
         banks = [(j, g, h) for j in (2, 3) for g in range(NG) for h in range(2)]
-        ctx.enter_context(tc.manual_schedule(engines={mybir.EngineType.DVE, mybir.EngineType.Pool, mybir.EngineType.PE}))
+        ctx.enter_context(tc.manual_schedule(engines={mybir.EngineType.DVE, mybir.EngineType.Pool, mybir.EngineType.PE, mybir.EngineType.Activation}))
         for m in range(NM):
             mm("k", 0, m, (0, 1), False)
         for m in range(NM):

@@ -181,12 +181,13 @@ def tile_llamaattention_pa_kernel(tc, x, Wq_bytes, Wq_scale, Wk, rope_cos, rope_
         ld_x(1)
         ld_k(0, 3)
         ld_q(0, 3)
-        for j in (1, 2):
-            for g in range(NG):
-                ld_k(j, g)
-            for g in range(NG):
-                ld_q(j, g)
-        late_loads = [(ld_k, 3), (ld_q, 3)]
+        for g in range(NG):
+            ld_k(1, g)
+        for g in range(NG):
+            ld_q(1, g)
+        for g in range(NG):
+            ld_k(2, g)
+        late_loads = [(ld_q, 2), (ld_k, 3), (ld_q, 3)]
 
         warm = const.tile([P, 1], F32, name="warm")
         warm2 = const.tile([P, 1], F32, name="warm2")
@@ -253,7 +254,7 @@ def tile_llamaattention_pa_kernel(tc, x, Wq_bytes, Wq_scale, Wk, rope_cos, rope_
 
         seq = [(w, j) for j in range(NJ) for w in ("k", "q")]
         banks = [(j, g, h) for j in (2, 3) for g in range(NG) for h in range(2)]
-        ctx.enter_context(tc.manual_schedule(engines={mybir.EngineType.DVE, mybir.EngineType.Pool, mybir.EngineType.PE, mybir.EngineType.Activation}))
+        ctx.enter_context(tc.manual_schedule(engines={mybir.EngineType.DVE, mybir.EngineType.Pool, mybir.EngineType.PE, mybir.EngineType.Activation, mybir.EngineType.SP}))
         for m in range(NM):
             mm("k", 0, m, (0, 1), False)
         for m in range(NM):

@@ -301,9 +301,6 @@ def tile_llamaattention_pa_kernel(tc, x, Wq_bytes, Wq_scale, Wk, rope_cos, rope_
             jq, gq = (i + 1) // 2, (i - 1) % 2
             post = []
             if i >= 1 and jq < NJ:
-                for g in (2 * gq, 2 * gq + 1):
-                    if (jq, g) in Q_ON_VECTOR:
-                        post.append(("inter", "q", jq, g))
                 if i == len(seq) - 2:
                     post.append(("unit", "q", jq, 3))
                     post.append(("unit", "q", jq, 2))
@@ -318,6 +315,10 @@ def tile_llamaattention_pa_kernel(tc, x, Wq_bytes, Wq_scale, Wk, rope_cos, rope_
                 else:
                     post.append(("half", "k", u[0], u[1]))
             filled = [(cover[0][0], cover[0][1] // 2)] if cover else []
+            if js < NJ:
+                for g in (2 * hs, 2 * hs + 1):
+                    if (js, g) in Q_ON_VECTOR:
+                        post.append(("inter", "q", js, g))
             for n in range(len(post)):
                 kind, a, b, c = post[n]
                 if n == len(post) - 1:

@@ -288,9 +288,10 @@ def tile_llamaattention_pa_kernel(tc, x, Wq_bytes, Wq_scale, Wk, rope_cos, rope_
                     add(nc.gpsimd, w, j, m)
                     if m == 1:
                         store(w, j, 0)
-                if m < len(cover):
-                    pe_inter(*cover[m])
-                    empty("S", *cover[m])
+                if m == 0:
+                    for bank in cover:
+                        pe_inter(*bank)
+                        empty("S", *bank)
                 if nxt:
                     mm(nxt[0], nxt[1], m, early, not late)
             if late_loads:

@@ -273,9 +273,6 @@ def tile_llamaattention_pa_kernel(tc, x, Wq_bytes, Wq_scale, Wk, rope_cos, rope_
             if js < NJ:
                 for g in (2 * hs + 1, 2 * hs):
                     widen(js, g)
-                for g in (2 * hs, 2 * hs + 1):
-                    if (js, g) not in Q_ON_VECTOR:
-                        inter("S", "q", js, g)
             if held:
                 await_flag(i - 1)
                 add(nc.gpsimd, held[0], held[1], 2)
@@ -292,6 +289,10 @@ def tile_llamaattention_pa_kernel(tc, x, Wq_bytes, Wq_scale, Wk, rope_cos, rope_
                     for bank in cover:
                         pe_inter(*bank)
                         empty("S", *bank)
+                    if js < NJ:
+                        for g in (2 * hs, 2 * hs + 1):
+                            if (js, g) not in Q_ON_VECTOR:
+                                inter("S", "q", js, g)
                 if nxt:
                     mm(nxt[0], nxt[1], m, early, not late)
             if late_loads:

@@ -25,7 +25,8 @@ NJ = E // NC
 NM = (B * S) // P
 HC = NC // HD
 
-Q_ON_VECTOR = ((0, 0), (0, 1), (0, 2), (0, 3), (1, 3), (2, 1), (2, 3), (3, 3))
+Q_ON_VECTOR = ((0, 0), (0, 1), (0, 2), (0, 3), (1, 3), (2, 1), (2, 3))
+Q_ON_TENSOR = ((3, 3), (3, 2))
 COVER = (0, 4, 4, 4, 4, 0, 0, 0)
 
 
@@ -79,18 +80,18 @@ def tile_llamaattention_pa_kernel(tc, x, Wq_bytes, Wq_scale, Wk, rope_cos, rope_
             else:
                 nc.scalar.copy(out=dst, in_=view)
 
-        def pe_inter(j, g, h):
+        def pe_inter(j, g, h, w="k"):
             t = psum.tile([P, NC // 2, PACK], BF16, name="stg", tag="stg")
             for q in range(2):
                 c0 = h * 256 + q * 128
                 nc.tensor.matmul(out=t[:, q * 128:(q + 1) * 128, :], lhsT=identb[:],
-                                 rhs=src[("k", j, g)][:, :, c0:c0 + 128].rearrange("p t c -> p c t"),
+                                 rhs=src[(w, j, g)][:, :, c0:c0 + 128].rearrange("p t c -> p c t"),
                                  start=True, stop=True)
-            stage[(j, g, h)] = t
+            stage[(w, j, g, h)] = t
 
-        def empty(eng, j, g, h):
-            dst = il_of("k", j, g)[:, g % 2, h * 256:(h + 1) * 256, :].rearrange("p c t -> p (c t)").bitcast(F32)
-            words = stage[(j, g, h)][:].rearrange("p c t -> p (c t)").bitcast(F32)
+        def empty(eng, j, g, h, w="k"):
+            dst = il_of(w, j, g)[:, g % 2, h * 256:(h + 1) * 256, :].rearrange("p c t -> p (c t)").bitcast(F32)
+            words = stage[(w, j, g, h)][:].rearrange("p c t -> p (c t)").bitcast(F32)
             if eng == "V":
                 nc.vector.tensor_copy(out=dst, in_=words)
             else:
@@ -247,7 +248,7 @@ def tile_llamaattention_pa_kernel(tc, x, Wq_bytes, Wq_scale, Wk, rope_cos, rope_
             x_quant(1)
             inter("V", "q", 0, 3)
             quant("q", 0, 1)
-        for g in range(NG):
+        for g in range(2):
             for h in range(2):
                 pe_inter(1, g, h)
                 empty("S", 1, g, h)
@@ -291,7 +292,7 @@ def tile_llamaattention_pa_kernel(tc, x, Wq_bytes, Wq_scale, Wk, rope_cos, rope_
                         empty("S", *bank)
                     if js < NJ:
                         for g in (2 * hs, 2 * hs + 1):
-                            if (js, g) not in Q_ON_VECTOR:
+                            if (js, g) not in Q_ON_VECTOR and (js, g) not in Q_ON_TENSOR:
                                 inter("S", "q", js, g)
                 if nxt:
                     mm(nxt[0], nxt[1], m, early, not late)
@@ -309,6 +310,8 @@ def tile_llamaattention_pa_kernel(tc, x, Wq_bytes, Wq_scale, Wk, rope_cos, rope_
                 else:
                     post.append(("half", "q", jq, gq))
             if i == 0:
+                post.append(("inter", "k", 1, 2))
+                post.append(("inter", "k", 1, 3))
                 post.append(("half", "k", 1, 0))
                 post.append(("half", "k", 1, 1))
             for u in filled:
@@ -334,6 +337,12 @@ def tile_llamaattention_pa_kernel(tc, x, Wq_bytes, Wq_scale, Wk, rope_cos, rope_
             if late:
                 for m in range(NM):
                     mm(nxt[0], nxt[1], m, late, True)
+            if js < NJ:
+                for g in (2 * hs + 1, 2 * hs):
+                    if (js, g) in Q_ON_TENSOR:
+                        for h in range(2):
+                            pe_inter(js, g, h, "q")
+                            empty("S", js, g, h, "q")
             if last:
                 add(nc.vector, w, j, 2)
                 for h0 in (0, HC // 2):

@@ -182,10 +182,14 @@ def tile_llamaattention_pa_kernel(tc, x, Wq_bytes, Wq_scale, Wk, rope_cos, rope_
         ld_x(1)
         ld_k(0, 3)
         ld_q(0, 3)
-        for g in range(NG):
-            ld_k(1, g)
-        for g in range(NG):
-            ld_q(1, g)
+        ld_k(1, 0)
+        ld_k(1, 1)
+        ld_q(1, 1)
+        ld_q(1, 0)
+        ld_k(1, 2)
+        ld_k(1, 3)
+        ld_q(1, 3)
+        ld_q(1, 2)
         for g in range(NG):
             ld_k(2, g)
         late_loads = [(ld_q, 2), (ld_k, 3), (ld_q, 3)]
@@ -248,18 +252,22 @@ def tile_llamaattention_pa_kernel(tc, x, Wq_bytes, Wq_scale, Wk, rope_cos, rope_
             x_quant(1)
             inter("V", "q", 0, 3)
             quant("q", 0, 1)
-        for g in range(2):
-            for h in range(2):
-                pe_inter(1, g, h)
-                empty("S", 1, g, h)
 
         seq = [(w, j) for j in range(NJ) for w in ("k", "q")]
         banks = [(j, g, h) for j in (2, 3) for g in range(NG) for h in range(2)]
         ctx.enter_context(tc.manual_schedule(engines={mybir.EngineType.DVE, mybir.EngineType.Pool, mybir.EngineType.PE, mybir.EngineType.Activation, mybir.EngineType.SP}))
-        for m in range(NM):
-            mm("k", 0, m, (0, 1), False)
-        for m in range(NM):
-            mm("k", 0, m, (2, 3), True)
+        def k1_unit(g):
+            for h in range(2):
+                pe_inter(1, g, h)
+                empty("S", 1, g, h)
+        mm("k", 0, 0, (0, 1), False)
+        mm("k", 0, 1, (0, 1), False)
+        k1_unit(0)
+        k1_unit(1)
+        mm("k", 0, 0, (2, 3), True)
+        mm("k", 0, 1, (2, 3), True)
+        mm("k", 0, 2, (0, 1, 2, 3), True)
+        mm("k", 0, 3, (0, 1, 2, 3), True)
         filled = []
         held = None
         for i in range(len(seq)):

@@ -235,7 +235,7 @@ def tile_llamaattention_pa_kernel(tc, x, Wq_bytes, Wq_scale, Wk, rope_cos, rope_
             inter("V", "k", 0, 0)
             inter("V", "q", 0, 0)
             inter("V", "k", 0, 1)
-            inter("V", "q", 0, 1)
+            inter("S", "q", 0, 1)
             quant("k", 0, 0)
             quant("q", 0, 0)
             for g in range(NG):
@@ -263,11 +263,13 @@ def tile_llamaattention_pa_kernel(tc, x, Wq_bytes, Wq_scale, Wk, rope_cos, rope_
         mm("k", 0, 0, (0, 1), False)
         mm("k", 0, 1, (0, 1), False)
         k1_unit(0)
-        k1_unit(1)
         mm("k", 0, 0, (2, 3), True)
         mm("k", 0, 1, (2, 3), True)
         mm("k", 0, 2, (0, 1, 2, 3), True)
         mm("k", 0, 3, (0, 1, 2, 3), True)
+        widen(1, 1)
+        widen(1, 0)
+        k1_unit(1)
         filled = []
         held = None
         for i in range(len(seq)):
@@ -279,7 +281,7 @@ def tile_llamaattention_pa_kernel(tc, x, Wq_bytes, Wq_scale, Wk, rope_cos, rope_
             cover = banks[:COVER[i]]
             banks = banks[COVER[i]:]
             js, hs = i // 2 + 1, i % 2
-            if js < NJ:
+            if js < NJ and i > 0:
                 for g in (2 * hs + 1, 2 * hs):
                     widen(js, g)
             if held:

@@ -27,6 +27,7 @@ HC = NC // HD
 
 Q_ON_VECTOR = ((0, 0), (0, 1), (0, 2), (0, 3), (1, 3), (2, 1), (2, 3))
 Q_ON_TENSOR = ((3, 3), (3, 2))
+MX_ALIGN = 256
 COVER = (0, 4, 4, 4, 4, 0, 0, 0)
 
 
@@ -99,8 +100,8 @@ def tile_llamaattention_pa_kernel(tc, x, Wq_bytes, Wq_scale, Wk, rope_cos, rope_
 
         def codes_of(w, j):
             if (w, j) not in codes:
-                c = work.tile([P, NG, NC], U32, name=w + "c", tag=w + "c", bufs=2, align_bytes=64)
-                s = work.tile([P, NG, NC], U8, name=w + "s", tag=w + "s", bufs=2, align_bytes=64)
+                c = work.tile([P, NG, NC], U32, name=w + "c", tag=w + "c", bufs=2, align_bytes=MX_ALIGN)
+                s = work.tile([P, NG, NC], U8, name=w + "s", tag=w + "s", bufs=2, align_bytes=MX_ALIGN)
                 codes[(w, j)] = (c, s)
             return codes[(w, j)]
 
@@ -209,8 +210,8 @@ def tile_llamaattention_pa_kernel(tc, x, Wq_bytes, Wq_scale, Wk, rope_cos, rope_
         nc.vector.tensor_copy(out=tabv[:, :, 1, :, 0], in_=sin_sb[:])
         nc.vector.tensor_scalar(out=tabv[:, :, 1, :, 1], in0=sin_sb[:], scalar1=-1.0, scalar2=None, op0=ALU.mult)
 
-        xc = const.tile([P, B, NG, 2 * P], U32, name="xc", align_bytes=64)
-        xs = const.tile([P, B, NG, 2 * P], U8, name="xs", align_bytes=64)
+        xc = const.tile([P, B, NG, 2 * P], U32, name="xc", align_bytes=MX_ALIGN)
+        xs = const.tile([P, B, NG, 2 * P], U8, name="xs", align_bytes=MX_ALIGN)
         xg = {}
 
         def x_turn(b, g):

@@ -85,8 +85,8 @@ def tile_llamaattention_pa_kernel(tc, x, Wq_bytes, Wq_scale, Wk, rope_cos, rope_
             t = psum.tile([P, NC // 2, PACK], BF16, name="stg", tag="stg")
             for q in range(2):
                 c0 = h * 256 + q * 128
-                nc.tensor.matmul(out=t[:, q * 128:(q + 1) * 128, :], lhsT=identb[:],
-                                 rhs=src[(w, j, g)][:, :, c0:c0 + 128].rearrange("p t c -> p c t"),
+                nc.tensor.matmul(out=t[:, q * 128:(q + 1) * 128, :].rearrange("p (c i) t -> p c t i", i=4), lhsT=identb[:],
+                                 rhs=src[(w, j, g)][:, :, c0:c0 + 128].rearrange("p t (c i) -> p c t i", i=4),
                                  start=True, stop=True)
             stage[(w, j, g, h)] = t
 

@@ -27,6 +27,7 @@ HC = NC // HD
 
 Q_ON_VECTOR = ((0, 0), (0, 1), (0, 2), (0, 3), (1, 3), (2, 1), (2, 3))
 Q_ON_TENSOR = ((3, 3), (3, 2))
+RUN = 16
 MX_ALIGN = 256
 COVER = (0, 4, 4, 4, 4, 0, 0, 0)
 
@@ -85,8 +86,8 @@ def tile_llamaattention_pa_kernel(tc, x, Wq_bytes, Wq_scale, Wk, rope_cos, rope_
             t = psum.tile([P, NC // 2, PACK], BF16, name="stg", tag="stg")
             for q in range(2):
                 c0 = h * 256 + q * 128
-                nc.tensor.matmul(out=t[:, q * 128:(q + 1) * 128, :].rearrange("p (c i) t -> p c t i", i=4), lhsT=identb[:],
-                                 rhs=src[(w, j, g)][:, :, c0:c0 + 128].rearrange("p t (c i) -> p c t i", i=4),
+                nc.tensor.matmul(out=t[:, q * 128:(q + 1) * 128, :].rearrange("p (c i) t -> p c t i", i=RUN), lhsT=identb[:],
+                                 rhs=src[(w, j, g)][:, :, c0:c0 + 128].rearrange("p t (c i) -> p c t i", i=RUN),
                                  start=True, stop=True)
             stage[(w, j, g, h)] = t
 

@@ -133,10 +133,11 @@ def tile_llamaattention_pa_kernel(tc, x, Wq_bytes, Wq_scale, Wk, rope_cos, rope_
                                     start=(g == 0), stop=(closes and g == gs[-1]))
 
         def products(w, j, m):
-            shp = [P, 2, HC, HD]
-            t = work.tile(shp, F32, name="pab", tag="pab", bufs=6)
-            nc.vector.tensor_tensor(out=t[:], in0=tab[:, m % 2].unsqueeze(2).to_broadcast(shp),
-                                    in1=acc[(w, j, m)][:].rearrange("p (h d) -> p h d", h=HC).unsqueeze(1).to_broadcast(shp),
+            shp = [P, 2, HC, HD // 2, 2]
+            t = work.tile([P, 2, HC, HD], F32, name="pab", tag="pab", bufs=6)
+            nc.vector.tensor_tensor(out=t[:].rearrange("p a h (i r) -> p a h i r", r=2),
+                                    in0=tab[:, m % 2].rearrange("p a (i r) -> p a i r", r=2).unsqueeze(2).to_broadcast(shp),
+                                    in1=acc[(w, j, m)][:].rearrange("p (h i a) -> p a h i", h=HC, a=2).unsqueeze(4).to_broadcast(shp),
                                     op=ALU.mult)
             prod[(w, j, m)] = t
 
@@ -145,23 +146,16 @@ def tile_llamaattention_pa_kernel(tc, x, Wq_bytes, Wq_scale, Wk, rope_cos, rope_
             if (w, j, b) not in res:
                 res[(w, j, b)] = work.tile([P, HC, 2, HD], F32, name="r", tag="r")
             t = prod[(w, j, m)]
-            eng.tensor_tensor(out=res[(w, j, b)][:, h0:h1, e, :].rearrange("p h (i r) -> p h i r", r=2),
-                              in0=t[:, 0, h0:h1].rearrange("p h (i r) -> p h i r", r=2),
-                              in1=t[:, 1, h0:h1].rearrange("p h (i r) -> p h i r", r=2)[:, :, :, ::-1], op=ALU.add)
+            eng.tensor_tensor(out=res[(w, j, b)][:, h0:h1, e, :], in0=t[:, 0, h0:h1], in1=t[:, 1, h0:h1], op=ALU.add)
 
         def store(w, j, b, h0=0, h1=HC):
             nc.sync.dma_start(out=outs[w][b, j * HC + h0:j * HC + h1].rearrange("h (p e) d -> p h (e d)", e=2),
                               in_=res[(w, j, b)][:, h0:h1].rearrange("p h e d -> p h (e d)"))
 
-        sink = const.tile([P, 1], F32, name="sink")
-        flags = {}
 
-        def raise_flag(i):
-            flags[i] = work.tile([P, 1], F32, name="flag", tag="flag", bufs=2)
-            nc.vector.memset(flags[i][:], 0.0)
-
-        def await_flag(i):
-            nc.gpsimd.tensor_copy(out=sink[:], in_=flags[i][:])
+        def raise_flag(w, j):
+            res[(w, j, 1)] = work.tile([P, HC, 2, HD], F32, name="r", tag="r")
+            nc.vector.memset(res[(w, j, 1)][:, 0, 0, 0:1], 0.0)
 
         scl = const.tile([P, NG, PACK], F32, name="scl")
         x_sb = const.tile([P, B, 2, D], BF16, name="x_sb")
@@ -207,9 +201,9 @@ def tile_llamaattention_pa_kernel(tc, x, Wq_bytes, Wq_scale, Wk, rope_cos, rope_
         tab = const.tile([P, 2, 2, HD], F32, name="tab")
         tabv = tab[:].rearrange("p e f (i r) -> p e f i r", r=2)
         nc.vector.tensor_copy(out=tabv[:, :, 0, :, 0], in_=cos_sb[:])
-        nc.vector.tensor_copy(out=tabv[:, :, 0, :, 1], in_=cos_sb[:])
-        nc.vector.tensor_copy(out=tabv[:, :, 1, :, 0], in_=sin_sb[:])
-        nc.vector.tensor_scalar(out=tabv[:, :, 1, :, 1], in0=sin_sb[:], scalar1=-1.0, scalar2=None, op0=ALU.mult)
+        nc.vector.tensor_copy(out=tabv[:, :, 1, :, 1], in_=cos_sb[:])
+        nc.vector.tensor_copy(out=tabv[:, :, 0, :, 1], in_=sin_sb[:])
+        nc.vector.tensor_scalar(out=tabv[:, :, 1, :, 0], in0=sin_sb[:], scalar1=-1.0, scalar2=None, op0=ALU.mult)
 
         xc = const.tile([P, B, NG, 2 * P], U32, name="xc", align_bytes=MX_ALIGN)
         xs = const.tile([P, B, NG, 2 * P], U8, name="xs", align_bytes=MX_ALIGN)
@@ -287,7 +281,6 @@ def tile_llamaattention_pa_kernel(tc, x, Wq_bytes, Wq_scale, Wk, rope_cos, rope_
                 for g in (2 * hs + 1, 2 * hs):
                     widen(js, g)
             if held:
-                await_flag(i - 1)
                 add(nc.gpsimd, held[0], held[1], 2)
                 add(nc.gpsimd, held[0], held[1], 3)
                 store(held[0], held[1], 1)
@@ -339,7 +332,7 @@ def tile_llamaattention_pa_kernel(tc, x, Wq_bytes, Wq_scale, Wk, rope_cos, rope_
             for n in range(len(post)):
                 kind, a, b, c = post[n]
                 if n == len(post) - 1:
-                    raise_flag(i)
+                    raise_flag(w, j)
                 if kind == "inter":
                     inter("V", a, b, c)
                 elif kind == "half":

@@ -26,7 +26,7 @@ NM = (B * S) // P
 HC = NC // HD
 
 Q_ON_VECTOR = ((0, 0), (0, 1), (0, 2), (0, 3), (1, 3), (2, 1), (2, 3))
-Q_ON_TENSOR = ((3, 3), (3, 2))
+Q_ON_TENSOR = ((3, 3), (3, 2), (3, 1))
 RUN = 16
 MX_ALIGN = 256
 COVER = (0, 4, 4, 4, 4, 0, 0, 0)
@@ -74,26 +74,26 @@ def tile_llamaattention_pa_kernel(tc, x, Wq_bytes, Wq_scale, Wk, rope_cos, rope_
                 il[(w, j, g // 2)] = work.tile([P, 2, NC, PACK], BF16, name="il" + w, tag="il" + w, bufs=(3 if w == "k" else 2), align_bytes=64)
             return il[(w, j, g // 2)]
 
-        def inter(eng, w, j, g):
-            dst = il_of(w, j, g)[:, g % 2].rearrange("p (c i) t -> p c t i", i=4)
-            view = src[(w, j, g)][:].rearrange("p t (c i) -> p c t i", i=4)
+        def inter(eng, w, j, g, c0=0, c1=NC):
+            dst = il_of(w, j, g)[:, g % 2, c0:c1, :].rearrange("p (c i) t -> p c t i", i=4)
+            view = src[(w, j, g)][:, :, c0:c1].rearrange("p t (c i) -> p c t i", i=4)
             if eng == "V":
                 nc.vector.tensor_copy(out=dst, in_=view)
             else:
                 nc.scalar.copy(out=dst, in_=view)
 
-        def pe_inter(j, g, h, w="k"):
+        def pe_inter(j, g, h, w="k", nq=2):
             t = psum.tile([P, NC // 2, PACK], BF16, name="stg", tag="stg")
-            for q in range(2):
+            for q in range(nq):
                 c0 = h * 256 + q * 128
                 nc.tensor.matmul(out=t[:, q * 128:(q + 1) * 128, :].rearrange("p (c i) t -> p c t i", i=RUN), lhsT=identb[:],
                                  rhs=src[(w, j, g)][:, :, c0:c0 + 128].rearrange("p t (c i) -> p c t i", i=RUN),
                                  start=True, stop=True)
             stage[(w, j, g, h)] = t
 
-        def empty(eng, j, g, h, w="k"):
-            dst = il_of(w, j, g)[:, g % 2, h * 256:(h + 1) * 256, :].rearrange("p c t -> p (c t)").bitcast(F32)
-            words = stage[(w, j, g, h)][:].rearrange("p c t -> p (c t)").bitcast(F32)
+        def empty(eng, j, g, h, w="k", nq=2):
+            dst = il_of(w, j, g)[:, g % 2, h * 256:h * 256 + nq * 128, :].rearrange("p c t -> p (c t)").bitcast(F32)
+            words = stage[(w, j, g, h)][:, 0:nq * 128, :].rearrange("p c t -> p (c t)").bitcast(F32)
             if eng == "V":
                 nc.vector.tensor_copy(out=dst, in_=words)
             else:
@@ -121,7 +121,8 @@ def tile_llamaattention_pa_kernel(tc, x, Wq_bytes, Wq_scale, Wk, rope_cos, rope_
                                   in_=il[(w, j, gg)][:].rearrange("p g c t -> p (g c t)"))
 
         def mm(w, j, m, gs, closes):
-            if gs[0] == 0:
+            opens = (w, j, m) not in acc
+            if opens:
                 acc[(w, j, m)] = psum.tile([P, NC], F32, name="acc", tag="acc")
             t = acc[(w, j, m)]
             c, s = codes[(w, j)]
@@ -130,7 +131,7 @@ def tile_llamaattention_pa_kernel(tc, x, Wq_bytes, Wq_scale, Wk, rope_cos, rope_
                 nc.tensor.matmul_mx(out=t[:], lhsT=xc[:, b, g, e * P:(e + 1) * P].bitcast(FP8X4),
                                     lhsT_scale=xs[:, b, g, e * P:(e + 1) * P],
                                     rhs=c[:, g, :].bitcast(FP8X4), rhs_scale=s[:, g, :],
-                                    start=(g == 0), stop=(closes and g == gs[-1]))
+                                    start=(opens and g == gs[0]), stop=(closes and g == gs[-1]))
 
         def products(w, j, m):
             shp = [P, 2, HC, HD // 2, 2]
@@ -153,9 +154,9 @@ def tile_llamaattention_pa_kernel(tc, x, Wq_bytes, Wq_scale, Wk, rope_cos, rope_
                               in_=res[(w, j, b)][:, h0:h1].rearrange("p h e d -> p h (e d)"))
 
 
-        def raise_flag(w, j):
+        def raise_flag(w, j, waits_for, n):
             res[(w, j, 1)] = work.tile([P, HC, 2, HD], F32, name="r", tag="r")
-            nc.vector.memset(res[(w, j, 1)][:, 0, 0, 0:1], 0.0)
+            nc.vector.tensor_copy(out=res[(w, j, 1)][:, 0, 0, 0:n], in_=waits_for)
 
         scl = const.tile([P, NG, PACK], F32, name="scl")
         x_sb = const.tile([P, B, 2, D], BF16, name="x_sb")
@@ -274,12 +275,19 @@ def tile_llamaattention_pa_kernel(tc, x, Wq_bytes, Wq_scale, Wk, rope_cos, rope_
             nxt = None if last else seq[i + 1]
             early = () if last else tuple([g for g in range(NG) if (nxt[0], nxt[1], g) in ready])
             late = () if last else tuple([g for g in reversed(range(NG)) if g not in early])
+            if i == len(seq) - 2:
+                late = (0, 1)
             cover = banks[:COVER[i]]
             banks = banks[COVER[i]:]
             js, hs = i // 2 + 1, i % 2
-            if js < NJ and i > 0:
+            if js < NJ - 1 and i > 0:
                 for g in (2 * hs + 1, 2 * hs):
                     widen(js, g)
+            if i == 4:
+                widen(3, 3)
+            if i == 5:
+                widen(3, 0)
+                inter("S", "q", 3, 0)
             if held:
                 add(nc.gpsimd, held[0], held[1], 2)
                 add(nc.gpsimd, held[0], held[1], 3)
@@ -295,10 +303,13 @@ def tile_llamaattention_pa_kernel(tc, x, Wq_bytes, Wq_scale, Wk, rope_cos, rope_
                     for bank in cover:
                         pe_inter(*bank)
                         empty("S", *bank)
-                    if js < NJ:
+                    if js < NJ - 1:
                         for g in (2 * hs, 2 * hs + 1):
                             if (js, g) not in Q_ON_VECTOR and (js, g) not in Q_ON_TENSOR:
                                 inter("S", "q", js, g)
+                    if i == 4:
+                        widen(3, 2)
+                        widen(3, 1)
                 if nxt:
                     mm(nxt[0], nxt[1], m, early, not late)
             if late_loads:
@@ -310,8 +321,10 @@ def tile_llamaattention_pa_kernel(tc, x, Wq_bytes, Wq_scale, Wk, rope_cos, rope_
             post = []
             if i >= 1 and jq < NJ:
                 if i == len(seq) - 2:
-                    post.append(("unit", "q", jq, 3))
-                    post.append(("unit", "q", jq, 2))
+                    post.append(("unit", "q", jq, 0))
+                    post.append(("unit", "q", jq, 1))
+                elif i == len(seq) - 3:
+                    post.append(("half", "q", jq, 1))
                 else:
                     post.append(("half", "q", jq, gq))
             if i == 0:
@@ -332,7 +345,12 @@ def tile_llamaattention_pa_kernel(tc, x, Wq_bytes, Wq_scale, Wk, rope_cos, rope_
             for n in range(len(post)):
                 kind, a, b, c = post[n]
                 if n == len(post) - 1:
-                    raise_flag(w, j)
+                    if kind == "inter":
+                        raise_flag(w, j, src[(a, b, c)][:, PACK - 1, NC - 1:NC], 1)
+                    elif kind == "half":
+                        raise_flag(w, j, il[(a, b, c)][:, :, NC - 1, PACK - 1], 2)
+                    else:
+                        raise_flag(w, j, il[(a, b, c // 2)][:, c % 2, NC - 1, PACK - 1:PACK], 1)
                 if kind == "inter":
                     inter("V", a, b, c)
                 elif kind == "half":
@@ -342,12 +360,17 @@ def tile_llamaattention_pa_kernel(tc, x, Wq_bytes, Wq_scale, Wk, rope_cos, rope_
             if late:
                 for m in range(NM):
                     mm(nxt[0], nxt[1], m, late, True)
-            if js < NJ:
-                for g in (2 * hs + 1, 2 * hs):
-                    if (js, g) in Q_ON_TENSOR:
-                        for h in range(2):
-                            pe_inter(js, g, h, "q")
-                            empty("S", js, g, h, "q")
+            if i == 4:
+                for g in (3, 2):
+                    for h in range(2):
+                        pe_inter(3, g, h, "q")
+                        empty("S", 3, g, h, "q")
+            if i == 5:
+                pe_inter(3, 1, 0, "q")
+                empty("S", 3, 1, 0, "q")
+                pe_inter(3, 1, 1, "q", 1)
+                empty("S", 3, 1, 1, "q", 1)
+                inter("S", "q", 3, 1, 384, NC)
             if last:
                 add(nc.vector, w, j, 2)
                 for h0 in (0, HC // 2):

@@ -135,8 +135,13 @@ def tile_llamaattention_pa_kernel(tc, x, Wq_bytes, Wq_scale, Wk, rope_cos, rope_
 
         def products(w, j, m):
             shp = [P, 2, HC, HD // 2, 2]
-            t = work.tile([P, 2, HC, HD], F32, name="pab", tag="pab", bufs=6)
-            nc.vector.tensor_tensor(out=t[:].rearrange("p a h (i r) -> p a h i r", r=2),
+            if m < 2:
+                t = work.tile([P, 2, HC, 1, HD], F32, name="pab", tag="pab", bufs=2)
+            elif m == 2:
+                t = work.tile([P, 2, HC, 2, HD], F32, name="pcd", tag="pcd", bufs=2)
+            else:
+                t = prod[(w, j, 2)]
+            nc.vector.tensor_tensor(out=t[:, :, :, m % 2 if m >= 2 else 0, :].rearrange("p a h (i r) -> p a h i r", r=2),
                                     in0=tab[:, m % 2].rearrange("p a (i r) -> p a i r", r=2).unsqueeze(2).to_broadcast(shp),
                                     in1=acc[(w, j, m)][:].rearrange("p (h i a) -> p a h i", h=HC, a=2).unsqueeze(4).to_broadcast(shp),
                                     op=ALU.mult)
@@ -147,7 +152,12 @@ def tile_llamaattention_pa_kernel(tc, x, Wq_bytes, Wq_scale, Wk, rope_cos, rope_
             if (w, j, b) not in res:
                 res[(w, j, b)] = work.tile([P, HC, 2, HD], F32, name="r", tag="r")
             t = prod[(w, j, m)]
-            eng.tensor_tensor(out=res[(w, j, b)][:, h0:h1, e, :], in0=t[:, 0, h0:h1], in1=t[:, 1, h0:h1], op=ALU.add)
+            s = e if m >= 2 else 0
+            eng.tensor_tensor(out=res[(w, j, b)][:, h0:h1, e, :], in0=t[:, 0, h0:h1, s, :], in1=t[:, 1, h0:h1, s, :], op=ALU.add)
+
+        def add_pair(eng, w, j):
+            t = prod[(w, j, 2)]
+            eng.tensor_tensor(out=res[(w, j, 1)][:], in0=t[:, 0], in1=t[:, 1], op=ALU.add)
 
         def store(w, j, b, h0=0, h1=HC):
             nc.sync.dma_start(out=outs[w][b, j * HC + h0:j * HC + h1].rearrange("h (p e) d -> p h (e d)", e=2),
@@ -289,8 +299,7 @@ def tile_llamaattention_pa_kernel(tc, x, Wq_bytes, Wq_scale, Wk, rope_cos, rope_
                 widen(3, 0)
                 inter("S", "q", 3, 0)
             if held:
-                add(nc.gpsimd, held[0], held[1], 2)
-                add(nc.gpsimd, held[0], held[1], 3)
+                add_pair(nc.gpsimd, held[0], held[1])
                 store(held[0], held[1], 1)
             held = None if last else (w, j)
             for m in range(NM):

@@ -29,7 +29,8 @@ Q_ON_VECTOR = ((0, 0), (0, 1), (0, 2), (0, 3), (1, 3), (2, 1), (2, 3))
 Q_ON_TENSOR = ((3, 3), (3, 2), (3, 1))
 RUN = 16
 MX_ALIGN = 256
-COVER = (0, 4, 4, 4, 4, 0, 0, 0)
+COVER = (0, 4, 4, 4, 0, 0, 0, 0)
+V_RUNS = (4,)
 
 
 def tile_llamaattention_pa_kernel(tc, x, Wq_bytes, Wq_scale, Wk, rope_cos, rope_sin, out_0, out_1):
@@ -289,6 +290,10 @@ def tile_llamaattention_pa_kernel(tc, x, Wq_bytes, Wq_scale, Wk, rope_cos, rope_
                 late = (0, 1)
             cover = banks[:COVER[i]]
             banks = banks[COVER[i]:]
+            mine = []
+            if i in V_RUNS:
+                mine = [banks[0][:2], banks[2][:2]]
+                banks = banks[4:]
             js, hs = i // 2 + 1, i % 2
             if js < NJ - 1 and i > 0:
                 for g in (2 * hs + 1, 2 * hs):
@@ -312,6 +317,8 @@ def tile_llamaattention_pa_kernel(tc, x, Wq_bytes, Wq_scale, Wk, rope_cos, rope_
                     for bank in cover:
                         pe_inter(*bank)
                         empty("S", *bank)
+                    if mine:
+                        inter("S", "k", mine[1][0], mine[1][1])
                     if js < NJ - 1:
                         for g in (2 * hs, 2 * hs + 1):
                             if (js, g) not in Q_ON_VECTOR and (js, g) not in Q_ON_TENSOR:
@@ -347,6 +354,9 @@ def tile_llamaattention_pa_kernel(tc, x, Wq_bytes, Wq_scale, Wk, rope_cos, rope_
                 else:
                     post.append(("half", "k", u[0], u[1]))
             filled = [(cover[0][0], cover[0][1] // 2)] if cover else []
+            if mine:
+                post.append(("inter", "k", mine[0][0], mine[0][1]))
+                filled = [(mine[0][0], mine[0][1] // 2)]
             if js < NJ:
                 for g in (2 * hs, 2 * hs + 1):
                     if (js, g) in Q_ON_VECTOR:

@@ -385,11 +385,7 @@ def tile_llamaattention_pa_kernel(tc, x, Wq_bytes, Wq_scale, Wk, rope_cos, rope_
                         pe_inter(3, g, h, "q")
                         empty("S", 3, g, h, "q")
             if i == 5:
-                pe_inter(3, 1, 0, "q")
-                empty("S", 3, 1, 0, "q")
-                pe_inter(3, 1, 1, "q", 1)
-                empty("S", 3, 1, 1, "q", 1)
-                inter("S", "q", 3, 1, 384, NC)
+                inter("S", "q", 3, 1)
             if last:
                 add(nc.vector, w, j, 2)
                 for h0 in (0, HC // 2):

@@ -76,8 +76,8 @@ def tile_llamaattention_pa_kernel(tc, x, Wq_bytes, Wq_scale, Wk, rope_cos, rope_
             return il[(w, j, g // 2)]
 
         def inter(eng, w, j, g, c0=0, c1=NC):
-            dst = il_of(w, j, g)[:, g % 2, c0:c1, :].rearrange("p (c i) t -> p c t i", i=4)
-            view = src[(w, j, g)][:, :, c0:c1].rearrange("p t (c i) -> p c t i", i=4)
+            dst = il_of(w, j, g)[:, g % 2, c0:c1, :].rearrange("p (c i) t -> p c t i", i=8)
+            view = src[(w, j, g)][:, :, c0:c1].rearrange("p t (c i) -> p c t i", i=8)
             if eng == "V":
                 nc.vector.tensor_copy(out=dst, in_=view)
             else:

@@ -290,6 +290,10 @@ def tile_llamaattention_pa_kernel(tc, x, Wq_bytes, Wq_scale, Wk, rope_cos, rope_
                 late = (0, 1)
             cover = banks[:COVER[i]]
             banks = banks[COVER[i]:]
+            solo = None
+            if i == 2:
+                solo = cover[2][:2]
+                cover = cover[:2]
             mine = []
             if i in V_RUNS:
                 mine = [banks[0][:2], banks[2][:2]]
@@ -317,6 +321,8 @@ def tile_llamaattention_pa_kernel(tc, x, Wq_bytes, Wq_scale, Wk, rope_cos, rope_
                     for bank in cover:
                         pe_inter(*bank)
                         empty("S", *bank)
+                    if solo:
+                        inter("S", "k", solo[0], solo[1])
                     if mine:
                         inter("S", "k", mine[1][0], mine[1][1])
                     if js < NJ - 1:

@@ -38,8 +38,8 @@ def tile_llamaattention_pa_kernel(tc, x, Wq_bytes, Wq_scale, Wk, rope_cos, rope_
     outs = {"q": out_0, "k": out_1}
     with ExitStack() as ctx:
         const = ctx.enter_context(tc.tile_pool(name="const", bufs=1))
-        raw = ctx.enter_context(tc.tile_pool(name="raw", bufs=12))
         work = ctx.enter_context(tc.tile_pool(name="work", bufs=3))
+        raw = ctx.enter_context(tc.tile_pool(name="raw", bufs=12))
         psum = ctx.enter_context(tc.psum_pool(name="psum", bufs=4))
 
         wq_v = Wq_bytes.rearrange("(g p t) n -> g p t n", p=P, t=PACK)

from contextlib import ExitStack

import concourse.mybir as mybir
from concourse.masks import make_identity

F32 = mybir.dt.float32
BF16 = mybir.dt.bfloat16
U32 = mybir.dt.uint32
U8 = mybir.dt.uint8
FP8 = mybir.dt.float8_e4m3fn
FP8X4 = mybir.dt.float8_e4m3fn_x4
ALU = mybir.AluOpType
ACT = mybir.ActivationFunctionType

B, S, D, H, HD = 2, 256, 2048, 16, 128
E = H * HD
FLOPS = 2 * (B * S) * D * (2 * E)

P = 128
PACK = 4
KP = P * PACK
NG = D // KP
NC = 512
NJ = E // NC
NM = (B * S) // P
HC = NC // HD

Q_ON_VECTOR = ((0, 0), (0, 1), (0, 2), (0, 3), (1, 3), (2, 1), (2, 3))
Q_ON_TENSOR = ((3, 3), (3, 2), (3, 1))
RUN = 16
MX_ALIGN = 256
COVER = (0, 4, 4, 4, 0, 0, 0, 0)
V_RUNS = (4,)


def tile_llamaattention_pa_kernel(tc, x, Wq_bytes, Wq_scale, Wk, rope_cos, rope_sin, out_0, out_1):
    nc = tc.nc
    outs = {"q": out_0, "k": out_1}
    with ExitStack() as ctx:
        const = ctx.enter_context(tc.tile_pool(name="const", bufs=1))
        work = ctx.enter_context(tc.tile_pool(name="work", bufs=3))
        raw = ctx.enter_context(tc.tile_pool(name="raw", bufs=12))
        psum = ctx.enter_context(tc.psum_pool(name="psum", bufs=4))

        wq_v = Wq_bytes.rearrange("(g p t) n -> g p t n", p=P, t=PACK)
        wk_v = Wk.rearrange("(g p t) n -> g p t n", p=P, t=PACK)
        src = {}
        il = {}
        codes = {}
        stage = {}
        acc = {}
        prod = {}
        res = {}
        ready = []

        def ld_q(j, g):
            t = raw.tile([P, PACK, NC], U8, name="qbytes", tag="qbytes", bufs=8)
            nc.sync.dma_start(out=t[:], in_=wq_v[g, :, :, j * NC:(j + 1) * NC])
            src[("b", j, g)] = t

        def ld_k(j, g):
            t = raw.tile([P, PACK, NC], BF16, name="kraw", tag="kraw")
            nc.sync.dma_start(out=t[:], in_=wk_v[g, :, :, j * NC:(j + 1) * NC])
            src[("k", j, g)] = t

        def widen(j, g):
            t = work.tile([P, PACK, NC], BF16, name="wid", tag="wid")
            for k in range(PACK):
                nc.scalar.activation(out=t[:, k, :], in_=src[("b", j, g)][:, k, :].bitcast(FP8),
                                     func=ACT.Copy, scale=scl[:, g, k:k + 1])
            src[("q", j, g)] = t

        def il_of(w, j, g):
            if (w, j, g // 2) not in il:
                il[(w, j, g // 2)] = work.tile([P, 2, NC, PACK], BF16, name="il" + w, tag="il" + w, bufs=(3 if w == "k" else 2), align_bytes=64)
            return il[(w, j, g // 2)]

        def inter(eng, w, j, g, c0=0, c1=NC):
            dst = il_of(w, j, g)[:, g % 2, c0:c1, :].rearrange("p (c i) t -> p c t i", i=8)
            view = src[(w, j, g)][:, :, c0:c1].rearrange("p t (c i) -> p c t i", i=8)
            if eng == "V":
                nc.vector.tensor_copy(out=dst, in_=view)
            else:
                nc.scalar.copy(out=dst, in_=view)

        def pe_inter(j, g, h, w="k", nq=2):
            t = psum.tile([P, NC // 2, PACK], BF16, name="stg", tag="stg")
            for q in range(nq):
                c0 = h * 256 + q * 128
                nc.tensor.matmul(out=t[:, q * 128:(q + 1) * 128, :].rearrange("p (c i) t -> p c t i", i=RUN), lhsT=identb[:],
                                 rhs=src[(w, j, g)][:, :, c0:c0 + 128].rearrange("p t (c i) -> p c t i", i=RUN),
                                 start=True, stop=True)
            stage[(w, j, g, h)] = t

        def empty(eng, j, g, h, w="k", nq=2):
            dst = il_of(w, j, g)[:, g % 2, h * 256:h * 256 + nq * 128, :].rearrange("p c t -> p (c t)").bitcast(F32)
            words = stage[(w, j, g, h)][:, 0:nq * 128, :].rearrange("p c t -> p (c t)").bitcast(F32)
            if eng == "V":
                nc.vector.tensor_copy(out=dst, in_=words)
            else:
                nc.scalar.copy(out=dst, in_=words)

        def codes_of(w, j):
            if (w, j) not in codes:
                c = work.tile([P, NG, NC], U32, name=w + "c", tag=w + "c", bufs=2, align_bytes=MX_ALIGN)
                s = work.tile([P, NG, NC], U8, name=w + "s", tag=w + "s", bufs=2, align_bytes=MX_ALIGN)
                codes[(w, j)] = (c, s)
            return codes[(w, j)]

        def quant_unit(w, j, g):
            c, s = codes_of(w, j)
            ready.append((w, j, g))
            nc.vector.quantize_mx(out=c[:, g, :].bitcast(FP8X4), scales=s[:, g, :],
                                  in_=il[(w, j, g // 2)][:, g % 2].rearrange("p c t -> p (c t)"))

        def quant(w, j, gg):
            c, s = codes_of(w, j)
            ready.append((w, j, 2 * gg))
            ready.append((w, j, 2 * gg + 1))
            nc.vector.quantize_mx(out=c[:, 2 * gg:2 * gg + 2, :].rearrange("p g c -> p (g c)").bitcast(FP8X4),
                                  scales=s[:, 2 * gg:2 * gg + 2, :].rearrange("p g c -> p (g c)"),
                                  in_=il[(w, j, gg)][:].rearrange("p g c t -> p (g c t)"))

        def mm(w, j, m, gs, closes):
            opens = (w, j, m) not in acc
            if opens:
                acc[(w, j, m)] = psum.tile([P, NC], F32, name="acc", tag="acc")
            t = acc[(w, j, m)]
            c, s = codes[(w, j)]
            b, e = m // 2, m % 2
            for g in gs:
                nc.tensor.matmul_mx(out=t[:], lhsT=xc[:, b, g, e * P:(e + 1) * P].bitcast(FP8X4),
                                    lhsT_scale=xs[:, b, g, e * P:(e + 1) * P],
                                    rhs=c[:, g, :].bitcast(FP8X4), rhs_scale=s[:, g, :],
                                    start=(opens and g == gs[0]), stop=(closes and g == gs[-1]))

        def products(w, j, m):
            shp = [P, 2, HC, HD // 2, 2]
            if m < 2:
                t = work.tile([P, 2, HC, 1, HD], F32, name="pab", tag="pab", bufs=2)
            elif m == 2:
                t = work.tile([P, 2, HC, 2, HD], F32, name="pcd", tag="pcd", bufs=2)
            else:
                t = prod[(w, j, 2)]
            nc.vector.tensor_tensor(out=t[:, :, :, m % 2 if m >= 2 else 0, :].rearrange("p a h (i r) -> p a h i r", r=2),
                                    in0=tab[:, m % 2].rearrange("p a (i r) -> p a i r", r=2).unsqueeze(2).to_broadcast(shp),
                                    in1=acc[(w, j, m)][:].rearrange("p (h i a) -> p a h i", h=HC, a=2).unsqueeze(4).to_broadcast(shp),
                                    op=ALU.mult)
            prod[(w, j, m)] = t

        def add(eng, w, j, m, h0=0, h1=HC):
            b, e = m // 2, m % 2
            if (w, j, b) not in res:
                res[(w, j, b)] = work.tile([P, HC, 2, HD], F32, name="r", tag="r")
            t = prod[(w, j, m)]
            s = e if m >= 2 else 0
            eng.tensor_tensor(out=res[(w, j, b)][:, h0:h1, e, :], in0=t[:, 0, h0:h1, s, :], in1=t[:, 1, h0:h1, s, :], op=ALU.add)

        def add_pair(eng, w, j):
            t = prod[(w, j, 2)]
            eng.tensor_tensor(out=res[(w, j, 1)][:], in0=t[:, 0], in1=t[:, 1], op=ALU.add)

        def store(w, j, b, h0=0, h1=HC):
            nc.sync.dma_start(out=outs[w][b, j * HC + h0:j * HC + h1].rearrange("h (p e) d -> p h (e d)", e=2),
                              in_=res[(w, j, b)][:, h0:h1].rearrange("p h e d -> p h (e d)"))


        def raise_flag(w, j, waits_for, n):
            res[(w, j, 1)] = work.tile([P, HC, 2, HD], F32, name="r", tag="r")
            nc.vector.tensor_copy(out=res[(w, j, 1)][:, 0, 0, 0:n], in_=waits_for)

        scl = const.tile([P, NG, PACK], F32, name="scl")
        x_sb = const.tile([P, B, 2, D], BF16, name="x_sb")
        cos_sb = const.tile([P, 2, HD // 2], BF16, name="cos_sb")
        sin_sb = const.tile([P, 2, HD // 2], BF16, name="sin_sb")

        def ld_x(b):
            nc.sync.dma_start(out=x_sb[:, b, :, :], in_=x[b].rearrange("(p e) k -> p e k", e=2))

        nc.scalar.dma_start(out=scl[:], in_=Wq_scale.rearrange("(g p t) o -> p g (t o)", p=P, t=PACK))
        nc.scalar.dma_start(out=cos_sb[:], in_=rope_cos.rearrange("(p e) i -> p e i", e=2))
        nc.scalar.dma_start(out=sin_sb[:], in_=rope_sin.rearrange("(p e) i -> p e i", e=2))
        ld_q(0, 0)
        ld_k(0, 0)
        ld_q(0, 1)
        ld_k(0, 1)
        ld_x(0)
        ld_k(0, 2)
        ld_q(0, 2)
        ld_x(1)
        ld_k(0, 3)
        ld_q(0, 3)
        ld_k(1, 0)
        ld_k(1, 1)
        ld_q(1, 1)
        ld_q(1, 0)
        ld_k(1, 2)
        ld_k(1, 3)
        ld_q(1, 3)
        ld_q(1, 2)
        for g in range(NG):
            ld_k(2, g)
        late_loads = [(ld_q, 2), (ld_k, 3), (ld_q, 3)]

        warm = const.tile([P, 1], F32, name="warm")
        warm2 = const.tile([P, 1], F32, name="warm2")
        nc.vector.memset(warm[:], 0.0)
        nc.scalar.activation(out=warm2[:], in_=warm[:], func=ACT.Copy)
        ident = const.tile([P, P], F32, name="ident")
        make_identity(nc, ident[:])
        identb = const.tile([P, P], BF16, name="identb")
        make_identity(nc, identb[:])
        tab = const.tile([P, 2, 2, HD], F32, name="tab")
        tabv = tab[:].rearrange("p e f (i r) -> p e f i r", r=2)
        nc.vector.tensor_copy(out=tabv[:, :, 0, :, 0], in_=cos_sb[:])
        nc.vector.tensor_copy(out=tabv[:, :, 1, :, 1], in_=cos_sb[:])
        nc.vector.tensor_copy(out=tabv[:, :, 0, :, 1], in_=sin_sb[:])
        nc.vector.tensor_scalar(out=tabv[:, :, 1, :, 0], in0=sin_sb[:], scalar1=-1.0, scalar2=None, op0=ALU.mult)

        xc = const.tile([P, B, NG, 2 * P], U32, name="xc", align_bytes=MX_ALIGN)
        xs = const.tile([P, B, NG, 2 * P], U8, name="xs", align_bytes=MX_ALIGN)
        xg = {}

        def x_turn(b, g):
            if g == 0:
                xg[b] = work.tile([P, NG, 2 * P * PACK], BF16, name="xg", tag="xg", bufs=2, align_bytes=64)
            xt = psum.tile([P, 2, 2, P], F32, name="xt", tag="acc")
            for e in range(2):
                words = x_sb[:, b, e, :].bitcast(F32)
                for u in range(2):
                    nc.tensor.transpose(xt[:, e, u, :], words[:, 256 * g + u:256 * (g + 1):2], ident[:])
            nc.scalar.copy(out=xg[b][:, g, :].bitcast(F32).rearrange("p (e r u) -> p e r u", e=2, u=2),
                           in_=xt[:].rearrange("p e u r -> p e r u"))

        def x_quant(b):
            nc.vector.quantize_mx(out=xc[:, b].rearrange("p g c -> p (g c)").bitcast(FP8X4),
                                  scales=xs[:, b].rearrange("p g c -> p (g c)"),
                                  in_=xg[b][:].rearrange("p g c -> p (g c)"))

        with tc.manual_schedule(engines={mybir.EngineType.DVE}):
            widen(0, 0)
            widen(0, 1)
            inter("V", "k", 0, 0)
            inter("V", "q", 0, 0)
            inter("V", "k", 0, 1)
            inter("S", "q", 0, 1)
            quant("k", 0, 0)
            quant("q", 0, 0)
            for g in range(NG):
                x_turn(0, g)
            widen(0, 2)
            inter("V", "k", 0, 2)
            x_quant(0)
            inter("V", "q", 0, 2)
            for g in range(NG):
                x_turn(1, g)
            widen(0, 3)
            inter("V", "k", 0, 3)
            quant("k", 0, 1)
            x_quant(1)
            inter("V", "q", 0, 3)
            quant("q", 0, 1)

        seq = [(w, j) for j in range(NJ) for w in ("k", "q")]
        banks = [(j, g, h) for j in (2, 3) for g in range(NG) for h in range(2)]
        ctx.enter_context(tc.manual_schedule(engines={mybir.EngineType.DVE, mybir.EngineType.Pool, mybir.EngineType.PE, mybir.EngineType.Activation, mybir.EngineType.SP}))
        def k1_unit(g):
            for h in range(2):
                pe_inter(1, g, h)
                empty("S", 1, g, h)
        mm("k", 0, 0, (0, 1), False)
        mm("k", 0, 1, (0, 1), False)
        k1_unit(0)
        mm("k", 0, 0, (2, 3), True)
        mm("k", 0, 1, (2, 3), True)
        mm("k", 0, 2, (0, 1, 2, 3), True)
        mm("k", 0, 3, (0, 1, 2, 3), True)
        widen(1, 1)
        widen(1, 0)
        k1_unit(1)
        filled = []
        held = None
        for i in range(len(seq)):
            w, j = seq[i]
            last = i == len(seq) - 1
            nxt = None if last else seq[i + 1]
            early = () if last else tuple([g for g in range(NG) if (nxt[0], nxt[1], g) in ready])
            late = () if last else tuple([g for g in reversed(range(NG)) if g not in early])
            if i == len(seq) - 2:
                late = (0, 1)
            cover = banks[:COVER[i]]
            banks = banks[COVER[i]:]
            solo = None
            if i == 2:
                solo = cover[2][:2]
                cover = cover[:2]
            mine = []
            if i in V_RUNS:
                mine = [banks[0][:2], banks[2][:2]]
                banks = banks[4:]
            js, hs = i // 2 + 1, i % 2
            if js < NJ - 1 and i > 0:
                for g in (2 * hs + 1, 2 * hs):
                    widen(js, g)
            if i == 4:
                widen(3, 3)
            if i == 5:
                widen(3, 0)
                inter("S", "q", 3, 0)
            if held:
                add_pair(nc.gpsimd, held[0], held[1])
                store(held[0], held[1], 1)
            held = None if last else (w, j)
            for m in range(NM):
                products(w, j, m)
                if m < 2:
                    add(nc.gpsimd, w, j, m)
                    if m == 1:
                        store(w, j, 0)
                if m == 0:
                    for bank in cover:
                        pe_inter(*bank)
                        empty("S", *bank)
                    if solo:
                        inter("S", "k", solo[0], solo[1])
                    if mine:
                        inter("S", "k", mine[1][0], mine[1][1])
                    if js < NJ - 1:
                        for g in (2 * hs, 2 * hs + 1):
                            if (js, g) not in Q_ON_VECTOR and (js, g) not in Q_ON_TENSOR:
                                inter("S", "q", js, g)
                    if i == 4:
                        widen(3, 2)
                        widen(3, 1)
                if nxt:
                    mm(nxt[0], nxt[1], m, early, not late)
            if late_loads:
                fn, jj = late_loads[0]
                late_loads = late_loads[1:]
                for g in range(NG):
                    fn(jj, g)
            jq, gq = (i + 1) // 2, (i - 1) % 2
            post = []
            if i >= 1 and jq < NJ:
                if i == len(seq) - 2:
                    post.append(("unit", "q", jq, 0))
                    post.append(("unit", "q", jq, 1))
                elif i == len(seq) - 3:
                    post.append(("half", "q", jq, 1))
                else:
                    post.append(("half", "q", jq, gq))
            if i == 0:
                post.append(("inter", "k", 1, 2))
                post.append(("inter", "k", 1, 3))
                post.append(("half", "k", 1, 0))
                post.append(("half", "k", 1, 1))
            for u in filled:
                if nxt and nxt[0] == "k":
                    post = [("half", "k", u[0], u[1])] + post
                else:
                    post.append(("half", "k", u[0], u[1]))
            filled = [(cover[0][0], cover[0][1] // 2)] if cover else []
            if mine:
                post.append(("inter", "k", mine[0][0], mine[0][1]))
                filled = [(mine[0][0], mine[0][1] // 2)]
            if js < NJ:
                for g in (2 * hs, 2 * hs + 1):
                    if (js, g) in Q_ON_VECTOR:
                        post.append(("inter", "q", js, g))
            for n in range(len(post)):
                kind, a, b, c = post[n]
                if n == len(post) - 1:
                    if kind == "inter":
                        raise_flag(w, j, src[(a, b, c)][:, PACK - 1, NC - 1:NC], 1)
                    elif kind == "half":
                        raise_flag(w, j, il[(a, b, c)][:, :, NC - 1, PACK - 1], 2)
                    else:
                        raise_flag(w, j, il[(a, b, c // 2)][:, c % 2, NC - 1, PACK - 1:PACK], 1)
                if kind == "inter":
                    inter("V", a, b, c)
                elif kind == "half":
                    quant(a, b, c)
                else:
                    quant_unit(a, b, c)
            if late:
                for m in range(NM):
                    mm(nxt[0], nxt[1], m, late, True)
            if i == 4:
                for g in (3, 2):
                    for h in range(2):
                        pe_inter(3, g, h, "q")
                        empty("S", 3, g, h, "q")
            if i == 5:
                inter("S", "q", 3, 1)
            if last:
                add(nc.vector, w, j, 2)
                for h0 in (0, HC // 2):
                    add(nc.vector, w, j, 3, h0, h0 + HC // 2)
                    store(w, j, 1, h0, h0 + HC // 2)
